import numpy as np
import ml_dtypes


def mxq(x, axis, fmt="e4m3"):
    dtype, down = {"e4m3": (ml_dtypes.float8_e4m3fn, 7), "e5m2": (ml_dtypes.float8_e5m2, 14)}[fmt]
    v = np.moveaxis(np.asarray(x, np.float32).astype(ml_dtypes.bfloat16).astype(np.float64), axis, -1)
    blocks = v.reshape(v.shape[:-1] + (-1, 32))
    amax = np.abs(blocks).max(-1, keepdims=True)
    byte = np.maximum(np.where(amax > 0, np.frexp(amax)[1] - 1 + 127, 0) - down, 1)
    scale = np.exp2(byte - 127.0)
    codes = (blocks / scale).astype(np.float32).astype(dtype).astype(np.float64)
    return np.moveaxis((codes * scale).reshape(v.shape), -1, axis)


WIDE = False


def mx_kscale(k):
    if not WIDE:
        return np.ones(k)
    levels = np.array([10, -10, 5, -5, 0])
    a = np.random.permutation(np.resize(levels, k // 512 * 4)).reshape(k // 512, 4)
    idx = np.arange(k)
    return np.exp2(a[idx // 512, idx % 128 // 32])


BF16 = ml_dtypes.bfloat16


def bf(x):
    return np.asarray(x, np.float32).astype(BF16)


def f64(x):
    return np.asarray(x).astype(np.float64)


B, L, DIMIN, WIDTH, N_HEADS, N_EMBDS = 8, 1024, 128, 512, 8, 64
EPS = 1e-6
XS = 10.0
SD = np.sqrt(DIMIN / WIDTH)


def setup_inputs():
    s = mx_kscale(WIDTH)
    t = mx_kscale(WIDTH)
    return {"o": bf(np.random.standard_normal((B, L, WIDTH)) * 0.6 * s),
            "o_w": bf(np.random.standard_normal((WIDTH, WIDTH)) * 0.5 / np.sqrt(WIDTH) / s[None, :] * t[:, None]),
            "o_b": bf(np.random.standard_normal(WIDTH) * 0.1 * t),
            "D": bf(np.random.standard_normal((WIDTH, DIMIN)) * SD / t[:, None]),
            "x": bf(np.random.standard_normal((B, L, DIMIN)) * XS)}


def reference(o, o_w, o_b, D, x):
    xc = f64(x)
    d_target = (mxq(f64(o), 2, "e4m3") @ mxq(f64(o_w), 1, "e4m3").T) + f64(o_b)
    z_pred_ = np.maximum(d_target, 0.0)
    Dz = mxq(z_pred_, 2, "e4m3") @ mxq(f64(D), 0, "e4m3")
    Dz_norm = np.sqrt(np.sum(Dz * Dz, axis=-1, keepdims=True)) + EPS
    proj_scale = np.sum(Dz * xc, axis=-1, keepdims=True) / np.square(Dz_norm)
    z_pred = z_pred_ * proj_scale
    x_pred = proj_scale * Dz
    return z_pred, x_pred

@@ -1,0 +1,288 @@
+from contextlib import ExitStack
+
+import concourse.mybir as mybir
+from concourse.masks import make_identity
+
+F32 = mybir.dt.float32
+BF16 = mybir.dt.bfloat16
+U32 = mybir.dt.uint32
+U8 = mybir.dt.uint8
+FP8X4 = mybir.dt.float8_e4m3fn_x4
+ACT = mybir.ActivationFunctionType
+ALU = mybir.AluOpType
+
+P = 128
+NT = 64
+UT = 4
+NU = NT // UT
+EPS = 1e-6
+FLOPS = 2 * 8192 * 512 * 512 + 2 * 8192 * 512 * 128
+
+PIN = True
+ENG = {"a0":"v","a1":"s","b0":"s","b1":"s","b2":"s","b3":"v","e0":"v","e1":"s","e2":"s","e3":"s","xp":"v"}
+ORDER = [["a0",0],["a1",0],["c2",2],["b0",1],["b1",1],["b2",1],["qc",3],["dot",4],["qa",0],["p",4],["b3",1],["d",3],["sq",3],["xp",4],["e0",4],["e1",4],["e2",4],["e3",4],["st",4]]
+O_CHUNKS = [4, 4, 8, 8, 8, 8, 8, 8, 8]
+C2V = 0
+FINE = 99
+
+
+def tile_originaltemporalsae_pa_t_kernel(tc, o, o_w, o_b, D, x, out_0, out_1):
+    nc = tc.nc
+    o_v = o.flatten_outer_dims().rearrange("(p i) k -> p i k", i=NT)
+    x_v = x.flatten_outer_dims().rearrange("(p i) k -> p i k", i=NT)
+    z_v = out_0.flatten_outer_dims().rearrange("(p i) f -> p i f", i=NT)
+    xp_v = out_1.flatten_outer_dims().rearrange("(p i) f -> p i f", i=NT)
+
+    with ExitStack() as ctx:
+        const = ctx.enter_context(tc.tile_pool(name="const", bufs=1))
+        work = ctx.enter_context(tc.tile_pool(name="work", bufs=3))
+        psum = ctx.enter_context(tc.psum_pool(name="psum", bufs=8))
+        if PIN:
+            ctx.enter_context(tc.manual_schedule())
+
+        def bank():
+            return psum.tile([P, 512], F32, tag="bank", name="bank")
+
+        def eng_of(key, u):
+            e = ENG[key]
+            return e[u % len(e)]
+
+        eps = const.tile([P, 1], F32, name="eps")
+        nc.vector.memset(eps[:], EPS)
+        warm = const.tile([P, 1], F32, name="warm")
+        nc.scalar.activation(out=warm[:], in_=eps[:], func=ACT.Sqrt)
+        ident = const.tile([P, P], F32, name="ident")
+        make_identity(nc, ident[:])
+        bz = const.tile([P, P], BF16, name="bz")
+        nc.vector.memset(bz[:], 0.0)
+
+        w_sb = const.tile([P, 4, 512], BF16, name="w_sb")
+        nc.sync.dma_start(out=w_sb[:], in_=o_w.rearrange("(a p) k -> p a k", p=P))
+        nc.scalar.dma_start(out=bz[0:4, :], in_=o_b.rearrange("(t p) -> t p", p=P))
+        d_sb = const.tile([P, 4, P], BF16, name="d_sb")
+        nc.scalar.dma_start(out=d_sb[:], in_=D.rearrange("(t p) j -> p t j", p=P))
+
+        o_of = {}
+        x_of = {}
+        i0 = 0
+        xq = 0
+        for g, n in enumerate(O_CHUNKS):
+            och = const.tile([P, n, 512], BF16, name="och%d" % g)
+            nc.sync.dma_start(out=och[:], in_=o_v[:, i0 : i0 + n, :])
+            for l in range(n):
+                o_of[i0 + l] = och[:, l, :]
+            i0 += n
+            if g >= 1 and xq < 4:
+                xch = const.tile([P, 16, P], BF16, name="xch%d" % xq)
+                nc.sync.dma_start(out=xch[:], in_=x_v[:, 16 * xq : 16 * xq + 16, :])
+                for l in range(16):
+                    x_of[16 * xq + l] = xch[:, l, :]
+                xq += 1
+
+        def words_half(g, h, src0, src1, eng):
+            xt = bank()
+            for jj, src in enumerate((src0, src1)):
+                s32 = src.bitcast(F32)
+                for u in range(2):
+                    c = (2 * jj + u) * P
+                    nc.tensor.transpose(xt[:, c : c + P], s32[:, u * P : u * P + P], ident[:])
+            dst = g[:].bitcast(F32)[:, 512 * h : 512 * h + 512].rearrange("q (j r u) -> q j r u", j=2, u=2)
+            srcv = xt[:].rearrange("q (j u r) -> q j r u", j=2, u=2)
+            if eng == "s":
+                nc.scalar.copy(out=dst, in_=srcv)
+            else:
+                nc.vector.tensor_copy(out=dst, in_=srcv)
+
+        def quantise(pool, g, tag, width):
+            codes = pool.tile([P, width], U32, tag=tag + "c", name=tag + "c", align_bytes=64)
+            scales = pool.tile([P, width], U8, tag=tag + "s", name=tag + "s", align_bytes=64)
+            nc.vector.quantize_mx(out=codes[:].bitcast(FP8X4), scales=scales[:], in_=g)
+            return codes, scales
+
+        wg = work.tile([P, 2048], BF16, tag="g", name="wg", align_bytes=64)
+        words_half(wg, 0, w_sb[:, 0, :], w_sb[:, 1, :], "v")
+        words_half(wg, 1, w_sb[:, 2, :], w_sb[:, 3, :], "s")
+        wc, ws = quantise(const, wg[:], "w", 512)
+
+        bzf = const.tile([P, P], F32, name="bzf")
+        nc.vector.tensor_copy(out=bzf[:], in_=bz[:])
+        bt = bank()
+        nc.tensor.transpose(bt[:, 0:P], bzf[:], ident[:])
+        b_sb = const.tile([P, 4], F32, name="b_sb")
+        nc.vector.tensor_copy(out=b_sb[:], in_=bt[:, 0:4])
+
+        dg = const.tile([P, P, 4], BF16, name="dg", align_bytes=64)
+        nc.vector.tensor_copy(out=dg[:], in_=d_sb[:].rearrange("p t j -> p j t"))
+        dc, ds = quantise(const, dg[:].rearrange("p j t -> p (j t)"), "d", P)
+
+        st = {}
+
+        def stage_a(u, h):
+            if h == 0:
+                st["g", u] = work.tile([P, 2048], BF16, tag="g", name="g", align_bytes=64)
+            words_half(st["g", u], h, o_of[UT * u + 2 * h], o_of[UT * u + 2 * h + 1], eng_of("a%d" % h, u))
+
+        def stage_qa(u):
+            st["oc", u] = quantise(work, st["g", u][:], "o", 512)
+
+        def stage_b(u, ft):
+            oc, osc = st["oc", u]
+            if ft == 0:
+                st["rt", u] = work.tile([P, 4, 512], F32, tag="rt", name="rt", bufs=4)
+            rt = st["rt", u]
+            dt = bank()
+            nc.tensor.matmul_mx(
+                out=dt[:],
+                lhsT=wc[:, ft * P : ft * P + P].bitcast(FP8X4),
+                lhsT_scale=ws[:, ft * P : ft * P + P],
+                rhs=oc[:].bitcast(FP8X4),
+                rhs_scale=osc[:],
+                start=True,
+                stop=True,
+            )
+            if eng_of("b%d" % ft, u) == "s":
+                nc.scalar.activation(
+                    out=rt[:, ft, :], in_=dt[:], func=ACT.Relu, bias=b_sb[:, ft : ft + 1], scale=1.0
+                )
+            else:
+                nc.vector.tensor_scalar(
+                    out=rt[:, ft, :],
+                    in0=dt[:],
+                    scalar1=b_sb[:, ft : ft + 1],
+                    scalar2=0.0,
+                    op0=ALU.add,
+                    op1=ALU.max,
+                )
+
+        def stage_c2(u):
+            g2 = work.tile([P, 2048], BF16, tag="g2", name="g2", align_bytes=64)
+            dst = g2[:].rearrange("p (c t) -> p c t", t=4)
+            src = st["rt", u][:].rearrange("p t c -> p c t")
+            if u < C2V:
+                nc.vector.tensor_copy(out=dst, in_=src)
+            else:
+                nc.gpsimd.tensor_scalar(out=dst, in0=src, scalar1=1.0, scalar2=0.0, op0=ALU.mult, op1=ALU.add)
+            st["g2", u] = g2
+
+        def stage_qc(u):
+            st["rc", u] = quantise(work, st["g2", u][:], "r", 512)
+
+        def stage_d(u):
+            rc, rs = st["rc", u]
+            dz = bank()
+            for j in range(UT):
+                nc.tensor.matmul_mx(
+                    out=dz[:, j * P : j * P + P],
+                    lhsT=rc[:, j * P : j * P + P].bitcast(FP8X4),
+                    lhsT_scale=rs[:, j * P : j * P + P],
+                    rhs=dc[:].bitcast(FP8X4),
+                    rhs_scale=ds[:],
+                    start=True,
+                    stop=True,
+                )
+            st["dz", u] = dz
+
+        def stage_sq(u):
+            dz = st["dz", u]
+            n2 = work.tile([P, 4], F32, tag="n2", name="n2")
+            for j in range(UT):
+                junk_s = work.tile([P, P], F32, tag="junk_s", name="junk_s", bufs=2)
+                nc.scalar.activation(
+                    out=junk_s[:], in_=dz[:, j * P : j * P + P], func=ACT.Square, accum_out=n2[:, j : j + 1]
+                )
+            nr = work.tile([P, 4], F32, tag="nr", name="nr")
+            nc.scalar.activation(out=nr[:], in_=n2[:], func=ACT.Sqrt)
+            den = work.tile([P, 4], F32, tag="den", name="den")
+            nc.scalar.activation(out=den[:], in_=nr[:], func=ACT.Square, bias=eps[:, 0:1], scale=1.0)
+            st["den", u] = den
+
+        def stage_dot(u):
+            dz = st["dz", u]
+            s = work.tile([P, 4], F32, tag="s", name="s")
+            for j in range(UT):
+                junk_v = work.tile([P, P], F32, tag="junk_v", name="junk_v", bufs=2)
+                nc.vector.scalar_tensor_tensor(
+                    out=junk_v[:],
+                    in0=dz[:, j * P : j * P + P],
+                    scalar=1.0,
+                    in1=x_of[UT * u + j],
+                    op0=ALU.mult,
+                    op1=ALU.mult,
+                    accum_out=s[:, j : j + 1],
+                )
+            st["s", u] = s
+
+        def stage_p(u):
+            rec = work.tile([P, 4], F32, tag="rec", name="rec")
+            nc.vector.reciprocal(out=rec[:], in_=st["den", u][:])
+            pp = work.tile([P, 4], F32, tag="pp", name="pp")
+            nc.vector.tensor_tensor(out=pp[:], in0=st["s", u][:], in1=rec[:], op=ALU.mult)
+            st["pp", u] = pp
+
+        def stage_xp(u):
+            pp = st["pp", u]
+            dz = st["dz", u]
+            xp = work.tile([P, 4, P], F32, tag="xp", name="xp", bufs=4)
+            if eng_of("xp", u) == "s":
+                for j in range(UT):
+                    nc.scalar.activation(
+                        out=xp[:, j, :], in_=dz[:, j * P : j * P + P], func=ACT.Copy, scale=pp[:, j : j + 1]
+                    )
+            else:
+                nc.vector.tensor_tensor(
+                    out=xp[:],
+                    in0=dz[:].rearrange("p (j c) -> p j c", j=UT),
+                    in1=pp[:].unsqueeze(2).to_broadcast([P, UT, P]),
+                    op=ALU.mult,
+                )
+            st["xp", u] = xp
+
+        def stage_e(u, j):
+            rt = st["rt", u]
+            pp = st["pp", u]
+            if j == 0:
+                st["zs", u] = work.tile([P, 4, 512], F32, tag="zs", name="zs", bufs=4)
+            zs = st["zs", u]
+            zb = bank()
+            for ft in range(4):
+                nc.tensor.transpose(zb[:, ft * P : ft * P + P], rt[:, ft, j * P : j * P + P], ident[:])
+            if eng_of("e%d" % j, u) == "s":
+                nc.scalar.activation(out=zs[:, j, :], in_=zb[:], func=ACT.Copy, scale=pp[:, j : j + 1])
+            else:
+                nc.vector.tensor_scalar(
+                    out=zs[:, j, :], in0=zb[:], scalar1=pp[:, j : j + 1], scalar2=None, op0=ALU.mult
+                )
+            if u >= FINE:
+                nc.sync.dma_start(out=z_v[:, UT * u + j, :], in_=zs[:, j, :])
+
+        def stage_st(u):
+            if u < FINE:
+                nc.sync.dma_start(out=z_v[:, UT * u : UT * u + UT, :], in_=st["zs", u][:])
+            nc.sync.dma_start(out=xp_v[:, UT * u : UT * u + UT, :], in_=st["xp", u][:])
+
+        stages = {
+            "a0": lambda u: stage_a(u, 0),
+            "a1": lambda u: stage_a(u, 1),
+            "qa": stage_qa,
+            "b0": lambda u: stage_b(u, 0),
+            "b1": lambda u: stage_b(u, 1),
+            "b2": lambda u: stage_b(u, 2),
+            "b3": lambda u: stage_b(u, 3),
+            "c2": stage_c2,
+            "qc": stage_qc,
+            "d": stage_d,
+            "sq": stage_sq,
+            "dot": stage_dot,
+            "p": stage_p,
+            "xp": stage_xp,
+            "e0": lambda u: stage_e(u, 0),
+            "e1": lambda u: stage_e(u, 1),
+            "e2": lambda u: stage_e(u, 2),
+            "e3": lambda u: stage_e(u, 3),
+            "st": stage_st,
+        }
+        max_lag = max(lag for name, lag in ORDER)
+        for t in range(NU + max_lag):
+            for name, lag in ORDER:
+                if 0 <= t - lag < NU:
+                    stages[name](t - lag)

@@ -19,10 +19,10 @@ EPS = 1e-6
 FLOPS = 2 * 8192 * 512 * 512 + 2 * 8192 * 512 * 128
 
 PIN = True
-ENG = {"a0":"v","a1":"s","b0":"s","b1":"s","b2":"s","b3":"v","e0":"v","e1":"s","e2":"s","e3":"s","xp":"v"}
+ENG = {"a0":"s","a1":"s","b0":"s","b1":"s","b2":"s","b3":"v","e0":"v","e1":"s","e2":"s","e3":"s","xp":"v"}
 ORDER = [["a0",0],["a1",0],["c2",2],["b0",1],["b1",1],["b2",1],["qc",3],["dot",4],["qa",0],["p",4],["b3",1],["d",3],["sq",3],["xp",4],["e0",4],["e1",4],["e2",4],["e3",4],["st",4]]
 O_CHUNKS = [4, 4, 8, 8, 8, 8, 8, 8, 8]
-C2V = 0
+C2V = 16
 FINE = 99
 
 

@@ -19,7 +19,7 @@ EPS = 1e-6
 FLOPS = 2 * 8192 * 512 * 512 + 2 * 8192 * 512 * 128
 
 PIN = True
-ENG = {"a0":"s","a1":"s","b0":"s","b1":"s","b2":"s","b3":"v","e0":"v","e1":"s","e2":"s","e3":"s","xp":"v"}
+ENG = {"a0":"s","a1":"s","b0":"s","b1":"s","b2":"s","b3":"v","e0":"v","e1":"s","e2":"s","e3":"v","xp":"v"}
 ORDER = [["a0",0],["a1",0],["c2",2],["b0",1],["b1",1],["b2",1],["qc",3],["dot",4],["qa",0],["p",4],["b3",1],["d",3],["sq",3],["xp",4],["e0",4],["e1",4],["e2",4],["e3",4],["st",4]]
 O_CHUNKS = [4, 4, 8, 8, 8, 8, 8, 8, 8]
 C2V = 16

@@ -18,8 +18,8 @@ NU = NT // UT
 EPS = 1e-6
 FLOPS = 2 * 8192 * 512 * 512 + 2 * 8192 * 512 * 128
 
-PIN = True
-ENG = {"a0":"s","a1":"s","b0":"s","b1":"s","b2":"s","b3":"v","e0":"v","e1":"s","e2":"s","e3":"v","xp":"v"}
+PIN = False
+ENG = {"a0":"s","a1":"s","b0":"s","b1":"s","b2":"s","b3":"v","e0":"v","e1":"s","e2":"s","e3":"sv","xp":"v"}
 ORDER = [["a0",0],["a1",0],["c2",2],["b0",1],["b1",1],["b2",1],["qc",3],["dot",4],["qa",0],["p",4],["b3",1],["d",3],["sq",3],["xp",4],["e0",4],["e1",4],["e2",4],["e3",4],["st",4]]
 O_CHUNKS = [4, 4, 8, 8, 8, 8, 8, 8, 8]
 C2V = 16

@@ -18,12 +18,12 @@ NU = NT // UT
 EPS = 1e-6
 FLOPS = 2 * 8192 * 512 * 512 + 2 * 8192 * 512 * 128
 
-PIN = False
-ENG = {"a0":"s","a1":"s","b0":"s","b1":"s","b2":"s","b3":"v","e0":"v","e1":"s","e2":"s","e3":"sv","xp":"v"}
-ORDER = [["a0",0],["a1",0],["c2",2],["b0",1],["b1",1],["b2",1],["qc",3],["dot",4],["qa",0],["p",4],["b3",1],["d",3],["sq",3],["xp",4],["e0",4],["e1",4],["e2",4],["e3",4],["st",4]]
+PIN = True
+ENG = {"a0":"s","a1":"v","b0":"v","b1":"s","b2":"s","b3":"s","e0":"v","e1":"s","e2":"s","e3":"s","xp":"v"}
+ORDER = [["e0",4],["e1",4],["e2",4],["e3",4],["c2",2],["a0",0],["a1",0],["d",3],["sq",3],["xp",4],["st",4],["b0",1],["b1",1],["b2",1],["b3",1],["dot",3],["p",3],["Q",0]]
 O_CHUNKS = [4, 4, 8, 8, 8, 8, 8, 8, 8]
-C2V = 16
 FINE = 99
+C2 = "g"
 
 
 def tile_originaltemporalsae_pa_t_kernel(tc, o, o_w, o_b, D, x, out_0, out_1):
@@ -79,30 +79,26 @@ def tile_originaltemporalsae_pa_t_kernel(tc, o, o_w, o_b, D, x, out_0, out_1):
                     x_of[16 * xq + l] = xch[:, l, :]
                 xq += 1
 
-        def words_half(g, h, src0, src1, eng):
+        def words_half(g32, h, src0, src1, eng):
             xt = bank()
             for jj, src in enumerate((src0, src1)):
                 s32 = src.bitcast(F32)
                 for u in range(2):
                     c = (2 * jj + u) * P
                     nc.tensor.transpose(xt[:, c : c + P], s32[:, u * P : u * P + P], ident[:])
-            dst = g[:].bitcast(F32)[:, 512 * h : 512 * h + 512].rearrange("q (j r u) -> q j r u", j=2, u=2)
+            dst = g32[:, 512 * h : 512 * h + 512].rearrange("q (j r u) -> q j r u", j=2, u=2)
             srcv = xt[:].rearrange("q (j u r) -> q j r u", j=2, u=2)
             if eng == "s":
                 nc.scalar.copy(out=dst, in_=srcv)
             else:
                 nc.vector.tensor_copy(out=dst, in_=srcv)
 
-        def quantise(pool, g, tag, width):
-            codes = pool.tile([P, width], U32, tag=tag + "c", name=tag + "c", align_bytes=64)
-            scales = pool.tile([P, width], U8, tag=tag + "s", name=tag + "s", align_bytes=64)
-            nc.vector.quantize_mx(out=codes[:].bitcast(FP8X4), scales=scales[:], in_=g)
-            return codes, scales
-
-        wg = work.tile([P, 2048], BF16, tag="g", name="wg", align_bytes=64)
-        words_half(wg, 0, w_sb[:, 0, :], w_sb[:, 1, :], "v")
-        words_half(wg, 1, w_sb[:, 2, :], w_sb[:, 3, :], "s")
-        wc, ws = quantise(const, wg[:], "w", 512)
+        wg = const.tile([P, 2048], BF16, name="wg", align_bytes=64)
+        words_half(wg[:].bitcast(F32), 0, w_sb[:, 0, :], w_sb[:, 1, :], "v")
+        words_half(wg[:].bitcast(F32), 1, w_sb[:, 2, :], w_sb[:, 3, :], "s")
+        wc = const.tile([P, 512], U32, name="wc", align_bytes=64)
+        ws = const.tile([P, 512], U8, name="ws", align_bytes=64)
+        nc.vector.quantize_mx(out=wc[:].bitcast(FP8X4), scales=ws[:], in_=wg[:])
 
         bzf = const.tile([P, P], F32, name="bzf")
         nc.vector.tensor_copy(out=bzf[:], in_=bz[:])
@@ -113,20 +109,33 @@ def tile_originaltemporalsae_pa_t_kernel(tc, o, o_w, o_b, D, x, out_0, out_1):
 
         dg = const.tile([P, P, 4], BF16, name="dg", align_bytes=64)
         nc.vector.tensor_copy(out=dg[:], in_=d_sb[:].rearrange("p t j -> p j t"))
-        dc, ds = quantise(const, dg[:].rearrange("p j t -> p (j t)"), "d", P)
+        dc = const.tile([P, P], U32, name="dc", align_bytes=64)
+        ds = const.tile([P, P], U8, name="ds", align_bytes=64)
+        nc.vector.quantize_mx(out=dc[:].bitcast(FP8X4), scales=ds[:], in_=dg[:].rearrange("p j t -> p (j t)"))
 
         st = {}
 
-        def stage_a(u, h):
-            if h == 0:
-                st["g", u] = work.tile([P, 2048], BF16, tag="g", name="g", align_bytes=64)
-            words_half(st["g", u], h, o_of[UT * u + 2 * h], o_of[UT * u + 2 * h + 1], eng_of("a%d" % h, u))
+        def gg_of(r):
+            if ("gg", r) not in st:
+                st["gg", r] = work.tile([P, 4096], BF16, tag="gg", name="gg", bufs=1, align_bytes=64)
+            return st["gg", r]
 
-        def stage_qa(u):
-            st["oc", u] = quantise(work, st["g", u][:], "o", 512)
+        def stage_a(u, h):
+            g32 = gg_of(u)[:, 0:2048].bitcast(F32)
+            words_half(g32, h, o_of[UT * u + 2 * h], o_of[UT * u + 2 * h + 1], eng_of("a%d" % h, u))
+
+        def stage_q(r):
+            lo = 0 if r < NU else 512
+            hi = 1024 if r >= 2 else 512
+            cc = work.tile([P, 1024], U32, tag="cc", name="cc", align_bytes=64)
+            sc = work.tile([P, 1024], U8, tag="sc", name="sc", align_bytes=64)
+            nc.vector.quantize_mx(
+                out=cc[:, lo:hi].bitcast(FP8X4), scales=sc[:, lo:hi], in_=gg_of(r)[:, 4 * lo : 4 * hi]
+            )
+            st["cc", r] = (cc, sc)
 
         def stage_b(u, ft):
-            oc, osc = st["oc", u]
+            cc, sc = st["cc", u]
             if ft == 0:
                 st["rt", u] = work.tile([P, 4, 512], F32, tag="rt", name="rt", bufs=4)
             rt = st["rt", u]
@@ -135,8 +144,8 @@ def tile_originaltemporalsae_pa_t_kernel(tc, o, o_w, o_b, D, x, out_0, out_1):
                 out=dt[:],
                 lhsT=wc[:, ft * P : ft * P + P].bitcast(FP8X4),
                 lhsT_scale=ws[:, ft * P : ft * P + P],
-                rhs=oc[:].bitcast(FP8X4),
-                rhs_scale=osc[:],
+                rhs=cc[:, 0:512].bitcast(FP8X4),
+                rhs_scale=sc[:, 0:512],
                 start=True,
                 stop=True,
             )
@@ -155,26 +164,22 @@ def tile_originaltemporalsae_pa_t_kernel(tc, o, o_w, o_b, D, x, out_0, out_1):
                 )
 
         def stage_c2(u):
-            g2 = work.tile([P, 2048], BF16, tag="g2", name="g2", align_bytes=64)
-            dst = g2[:].rearrange("p (c t) -> p c t", t=4)
+            dst = gg_of(u + 2)[:, 2048:4096].rearrange("p (c t) -> p c t", t=4)
             src = st["rt", u][:].rearrange("p t c -> p c t")
-            if u < C2V:
+            if C2 == "v":
                 nc.vector.tensor_copy(out=dst, in_=src)
             else:
                 nc.gpsimd.tensor_scalar(out=dst, in0=src, scalar1=1.0, scalar2=0.0, op0=ALU.mult, op1=ALU.add)
-            st["g2", u] = g2
-
-        def stage_qc(u):
-            st["rc", u] = quantise(work, st["g2", u][:], "r", 512)
 
         def stage_d(u):
-            rc, rs = st["rc", u]
+            cc, sc = st["cc", u + 2]
             dz = bank()
             for j in range(UT):
+                c = 512 + j * P
                 nc.tensor.matmul_mx(
                     out=dz[:, j * P : j * P + P],
-                    lhsT=rc[:, j * P : j * P + P].bitcast(FP8X4),
-                    lhsT_scale=rs[:, j * P : j * P + P],
+                    lhsT=cc[:, c : c + P].bitcast(FP8X4),
+                    lhsT_scale=sc[:, c : c + P],
                     rhs=dc[:].bitcast(FP8X4),
                     rhs_scale=ds[:],
                     start=True,
@@ -263,13 +268,12 @@ def tile_originaltemporalsae_pa_t_kernel(tc, o, o_w, o_b, D, x, out_0, out_1):
         stages = {
             "a0": lambda u: stage_a(u, 0),
             "a1": lambda u: stage_a(u, 1),
-            "qa": stage_qa,
+            "Q": stage_q,
             "b0": lambda u: stage_b(u, 0),
             "b1": lambda u: stage_b(u, 1),
             "b2": lambda u: stage_b(u, 2),
             "b3": lambda u: stage_b(u, 3),
             "c2": stage_c2,
-            "qc": stage_qc,
             "d": stage_d,
             "sq": stage_sq,
             "dot": stage_dot,
@@ -282,7 +286,8 @@ def tile_originaltemporalsae_pa_t_kernel(tc, o, o_w, o_b, D, x, out_0, out_1):
             "st": stage_st,
         }
         max_lag = max(lag for name, lag in ORDER)
-        for t in range(NU + max_lag):
+        for t in range(NU + 2 + max_lag):
             for name, lag in ORDER:
-                if 0 <= t - lag < NU:
+                limit = NU + 2 if name == "Q" else NU
+                if 0 <= t - lag < limit:
                     stages[name](t - lag)

@@ -19,10 +19,10 @@ EPS = 1e-6
 FLOPS = 2 * 8192 * 512 * 512 + 2 * 8192 * 512 * 128
 
 PIN = True
-ENG = {"a0":"s","a1":"v","b0":"v","b1":"s","b2":"s","b3":"s","e0":"v","e1":"s","e2":"s","e3":"s","xp":"v"}
+ENG = {"a0":"s","a1":"v","b0":"v","b1":"s","b2":"s","b3":"s","e0":"v","e1":"sv","e2":"s","e3":"s","xp":"v"}
 ORDER = [["e0",4],["e1",4],["e2",4],["e3",4],["c2",2],["a0",0],["a1",0],["d",3],["sq",3],["xp",4],["st",4],["b0",1],["b1",1],["b2",1],["b3",1],["dot",3],["p",3],["Q",0]]
 O_CHUNKS = [4, 4, 8, 8, 8, 8, 8, 8, 8]
-FINE = 99
+FINE = 15
 C2 = "g"
 
 

@@ -12,282 +12,282 @@ ACT = mybir.ActivationFunctionType
 ALU = mybir.AluOpType
 
 P = 128
-NT = 64
-UT = 4
-NU = NT // UT
+K = 512
+PACK = 4
+TILES = 64
+UNIT = 4
+UNITS = TILES // UNIT
+BANK = 512
 EPS = 1e-6
-FLOPS = 2 * 8192 * 512 * 512 + 2 * 8192 * 512 * 128
+TINY = 1e-30
+FLOPS = 2 * 8192 * K * K + 2 * 8192 * K * P
 
-PIN = True
-ENG = {"a0":"s","a1":"v","b0":"v","b1":"s","b2":"s","b3":"s","e0":"v","e1":"sv","e2":"s","e3":"s","xp":"v"}
-ORDER = [["e0",4],["e1",4],["e2",4],["e3",4],["c2",2],["a0",0],["a1",0],["d",3],["sq",3],["xp",4],["st",4],["b0",1],["b1",1],["b2",1],["b3",1],["dot",3],["p",3],["Q",0]]
-O_CHUNKS = [4, 4, 8, 8, 8, 8, 8, 8, 8]
-FINE = 15
-C2 = "g"
+O_LOADS = [2, 2, 4, 8, 8, 8, 8, 8, 8, 8]
+X_LOAD = 16
 
 
 def tile_originaltemporalsae_pa_t_kernel(tc, o, o_w, o_b, D, x, out_0, out_1):
     nc = tc.nc
-    o_v = o.flatten_outer_dims().rearrange("(p i) k -> p i k", i=NT)
-    x_v = x.flatten_outer_dims().rearrange("(p i) k -> p i k", i=NT)
-    z_v = out_0.flatten_outer_dims().rearrange("(p i) f -> p i f", i=NT)
-    xp_v = out_1.flatten_outer_dims().rearrange("(p i) f -> p i f", i=NT)
+    o_v = o.flatten_outer_dims().rearrange("(p i) k -> p i k", i=TILES)
+    x_v = x.flatten_outer_dims().rearrange("(p i) k -> p i k", i=TILES)
+    z_v = out_0.flatten_outer_dims().rearrange("(p i) f -> p i f", i=TILES)
+    xp_v = out_1.flatten_outer_dims().rearrange("(p i) f -> p i f", i=TILES)
 
     with ExitStack() as ctx:
         const = ctx.enter_context(tc.tile_pool(name="const", bufs=1))
         work = ctx.enter_context(tc.tile_pool(name="work", bufs=3))
         psum = ctx.enter_context(tc.psum_pool(name="psum", bufs=8))
-        if PIN:
-            ctx.enter_context(tc.manual_schedule())
+        ctx.enter_context(tc.manual_schedule())
 
         def bank():
-            return psum.tile([P, 512], F32, tag="bank", name="bank")
-
-        def eng_of(key, u):
-            e = ENG[key]
-            return e[u % len(e)]
+            return psum.tile([P, BANK], F32, tag="bank", name="bank")
 
         eps = const.tile([P, 1], F32, name="eps")
         nc.vector.memset(eps[:], EPS)
+        tiny = const.tile([P, 1], F32, name="tiny")
+        nc.vector.memset(tiny[:], TINY)
         warm = const.tile([P, 1], F32, name="warm")
         nc.scalar.activation(out=warm[:], in_=eps[:], func=ACT.Sqrt)
         ident = const.tile([P, P], F32, name="ident")
         make_identity(nc, ident[:])
-        bz = const.tile([P, P], BF16, name="bz")
-        nc.vector.memset(bz[:], 0.0)
+        bias_rows = const.tile([P, P], BF16, name="bz")
+        nc.vector.memset(bias_rows[:], 0.0)
 
-        w_sb = const.tile([P, 4, 512], BF16, name="w_sb")
+        w_sb = const.tile([P, PACK, K], BF16, name="w_sb")
         nc.sync.dma_start(out=w_sb[:], in_=o_w.rearrange("(a p) k -> p a k", p=P))
-        nc.scalar.dma_start(out=bz[0:4, :], in_=o_b.rearrange("(t p) -> t p", p=P))
-        d_sb = const.tile([P, 4, P], BF16, name="d_sb")
+        nc.scalar.dma_start(out=bias_rows[0:PACK, :], in_=o_b.rearrange("(t p) -> t p", p=P))
+        d_sb = const.tile([P, PACK, P], BF16, name="d_sb")
         nc.scalar.dma_start(out=d_sb[:], in_=D.rearrange("(t p) j -> p t j", p=P))
 
-        o_of = {}
-        x_of = {}
-        i0 = 0
-        xq = 0
-        for g, n in enumerate(O_CHUNKS):
-            och = const.tile([P, n, 512], BF16, name="och%d" % g)
-            nc.sync.dma_start(out=och[:], in_=o_v[:, i0 : i0 + n, :])
+        o_tile = {}
+        x_tile = {}
+        first = 0
+        x_loads = 0
+        for g, n in enumerate(O_LOADS):
+            o_sb = const.tile([P, n, K], BF16, name="och%d" % g)
+            nc.sync.dma_start(out=o_sb[:], in_=o_v[:, first : first + n, :])
             for l in range(n):
-                o_of[i0 + l] = och[:, l, :]
-            i0 += n
-            if g >= 1 and xq < 4:
-                xch = const.tile([P, 16, P], BF16, name="xch%d" % xq)
-                nc.sync.dma_start(out=xch[:], in_=x_v[:, 16 * xq : 16 * xq + 16, :])
-                for l in range(16):
-                    x_of[16 * xq + l] = xch[:, l, :]
-                xq += 1
+                o_tile[first + l] = o_sb[:, l, :]
+            first += n
+            if g >= 2 and x_loads < TILES // X_LOAD:
+                x_sb = const.tile([P, X_LOAD, P], BF16, name="xch%d" % x_loads)
+                nc.sync.dma_start(out=x_sb[:], in_=x_v[:, X_LOAD * x_loads : X_LOAD * (x_loads + 1), :])
+                for l in range(X_LOAD):
+                    x_tile[X_LOAD * x_loads + l] = x_sb[:, l, :]
+                x_loads += 1
 
-        def words_half(g32, h, src0, src1, eng):
-            xt = bank()
-            for jj, src in enumerate((src0, src1)):
-                s32 = src.bitcast(F32)
+        def transpose_words(grouped32, half, rows0, rows1, on_scalar):
+            words = bank()
+            for j, rows in enumerate((rows0, rows1)):
+                rows32 = rows.bitcast(F32)
                 for u in range(2):
-                    c = (2 * jj + u) * P
-                    nc.tensor.transpose(xt[:, c : c + P], s32[:, u * P : u * P + P], ident[:])
-            dst = g32[:, 512 * h : 512 * h + 512].rearrange("q (j r u) -> q j r u", j=2, u=2)
-            srcv = xt[:].rearrange("q (j u r) -> q j r u", j=2, u=2)
-            if eng == "s":
-                nc.scalar.copy(out=dst, in_=srcv)
+                    c = (2 * j + u) * P
+                    nc.tensor.transpose(words[:, c : c + P], rows32[:, u * P : u * P + P], ident[:])
+            dst = grouped32[:, BANK * half : BANK * (half + 1)].rearrange("q (j r u) -> q j r u", j=2, u=2)
+            src = words[:].rearrange("q (j u r) -> q j r u", j=2, u=2)
+            if on_scalar:
+                nc.scalar.copy(out=dst, in_=src)
             else:
-                nc.vector.tensor_copy(out=dst, in_=srcv)
-
-        wg = const.tile([P, 2048], BF16, name="wg", align_bytes=64)
-        words_half(wg[:].bitcast(F32), 0, w_sb[:, 0, :], w_sb[:, 1, :], "v")
-        words_half(wg[:].bitcast(F32), 1, w_sb[:, 2, :], w_sb[:, 3, :], "s")
-        wc = const.tile([P, 512], U32, name="wc", align_bytes=64)
-        ws = const.tile([P, 512], U8, name="ws", align_bytes=64)
-        nc.vector.quantize_mx(out=wc[:].bitcast(FP8X4), scales=ws[:], in_=wg[:])
-
-        bzf = const.tile([P, P], F32, name="bzf")
-        nc.vector.tensor_copy(out=bzf[:], in_=bz[:])
-        bt = bank()
-        nc.tensor.transpose(bt[:, 0:P], bzf[:], ident[:])
-        b_sb = const.tile([P, 4], F32, name="b_sb")
-        nc.vector.tensor_copy(out=b_sb[:], in_=bt[:, 0:4])
-
-        dg = const.tile([P, P, 4], BF16, name="dg", align_bytes=64)
-        nc.vector.tensor_copy(out=dg[:], in_=d_sb[:].rearrange("p t j -> p j t"))
-        dc = const.tile([P, P], U32, name="dc", align_bytes=64)
-        ds = const.tile([P, P], U8, name="ds", align_bytes=64)
-        nc.vector.quantize_mx(out=dc[:].bitcast(FP8X4), scales=ds[:], in_=dg[:].rearrange("p j t -> p (j t)"))
-
-        st = {}
-
-        def gg_of(r):
-            if ("gg", r) not in st:
-                st["gg", r] = work.tile([P, 4096], BF16, tag="gg", name="gg", bufs=1, align_bytes=64)
-            return st["gg", r]
-
-        def stage_a(u, h):
-            g32 = gg_of(u)[:, 0:2048].bitcast(F32)
-            words_half(g32, h, o_of[UT * u + 2 * h], o_of[UT * u + 2 * h + 1], eng_of("a%d" % h, u))
-
-        def stage_q(r):
-            lo = 0 if r < NU else 512
-            hi = 1024 if r >= 2 else 512
-            cc = work.tile([P, 1024], U32, tag="cc", name="cc", align_bytes=64)
-            sc = work.tile([P, 1024], U8, tag="sc", name="sc", align_bytes=64)
-            nc.vector.quantize_mx(
-                out=cc[:, lo:hi].bitcast(FP8X4), scales=sc[:, lo:hi], in_=gg_of(r)[:, 4 * lo : 4 * hi]
-            )
-            st["cc", r] = (cc, sc)
-
-        def stage_b(u, ft):
-            cc, sc = st["cc", u]
-            if ft == 0:
-                st["rt", u] = work.tile([P, 4, 512], F32, tag="rt", name="rt", bufs=4)
-            rt = st["rt", u]
-            dt = bank()
-            nc.tensor.matmul_mx(
-                out=dt[:],
-                lhsT=wc[:, ft * P : ft * P + P].bitcast(FP8X4),
-                lhsT_scale=ws[:, ft * P : ft * P + P],
-                rhs=cc[:, 0:512].bitcast(FP8X4),
-                rhs_scale=sc[:, 0:512],
-                start=True,
-                stop=True,
-            )
-            if eng_of("b%d" % ft, u) == "s":
-                nc.scalar.activation(
-                    out=rt[:, ft, :], in_=dt[:], func=ACT.Relu, bias=b_sb[:, ft : ft + 1], scale=1.0
-                )
-            else:
-                nc.vector.tensor_scalar(
-                    out=rt[:, ft, :],
-                    in0=dt[:],
-                    scalar1=b_sb[:, ft : ft + 1],
-                    scalar2=0.0,
-                    op0=ALU.add,
-                    op1=ALU.max,
-                )
-
-        def stage_c2(u):
-            dst = gg_of(u + 2)[:, 2048:4096].rearrange("p (c t) -> p c t", t=4)
-            src = st["rt", u][:].rearrange("p t c -> p c t")
-            if C2 == "v":
                 nc.vector.tensor_copy(out=dst, in_=src)
-            else:
-                nc.gpsimd.tensor_scalar(out=dst, in0=src, scalar1=1.0, scalar2=0.0, op0=ALU.mult, op1=ALU.add)
 
-        def stage_d(u):
-            cc, sc = st["cc", u + 2]
-            dz = bank()
-            for j in range(UT):
-                c = 512 + j * P
+        w_grouped = const.tile([P, PACK * K], BF16, name="wg", align_bytes=64)
+        transpose_words(w_grouped[:].bitcast(F32), 0, w_sb[:, 0, :], w_sb[:, 1, :], False)
+        transpose_words(w_grouped[:].bitcast(F32), 1, w_sb[:, 2, :], w_sb[:, 3, :], True)
+        w_codes = const.tile([P, K], U32, name="wc", align_bytes=64)
+        w_scales = const.tile([P, K], U8, name="ws", align_bytes=64)
+        nc.vector.quantize_mx(out=w_codes[:].bitcast(FP8X4), scales=w_scales[:], in_=w_grouped[:])
+
+        bias_rows32 = const.tile([P, P], F32, name="bzf")
+        bias = const.tile([P, PACK], F32, name="b_sb")
+        d_grouped = const.tile([P, P, PACK], BF16, name="dg", align_bytes=64)
+        d_codes = const.tile([P, P], U32, name="dc", align_bytes=64)
+        d_scales = const.tile([P, P], U8, name="ds", align_bytes=64)
+
+        def prepare_bias_and_d():
+            nc.vector.tensor_copy(out=bias_rows32[:], in_=bias_rows[:])
+            bias_t = bank()
+            nc.tensor.transpose(bias_t[:, 0:P], bias_rows32[:], ident[:])
+            nc.vector.tensor_copy(out=bias[:], in_=bias_t[:, 0:PACK])
+            nc.vector.tensor_copy(out=d_grouped[:], in_=d_sb[:].rearrange("p t j -> p j t"))
+            nc.vector.quantize_mx(
+                out=d_codes[:].bitcast(FP8X4), scales=d_scales[:], in_=d_grouped[:].rearrange("p j t -> p (j t)")
+            )
+
+        grouped = {}
+        quantised = {}
+        r_t = {}
+        dz_bank = {}
+        denom = {}
+        dot = {}
+        scale = {}
+        z_sb = {}
+        xp_sb = {}
+
+        def grouped_of(t):
+            if t not in grouped:
+                grouped[t] = work.tile([P, 2 * PACK * K], BF16, tag="gg", name="gg", bufs=1, align_bytes=64)
+            return grouped[t]
+
+        def transpose_o(u):
+            grouped32 = grouped_of(u)[:, 0 : PACK * K].bitcast(F32)
+            transpose_words(grouped32, 0, o_tile[UNIT * u], o_tile[UNIT * u + 1], True)
+            transpose_words(grouped32, 1, o_tile[UNIT * u + 2], o_tile[UNIT * u + 3], False)
+
+        def quantise(t):
+            lo = 0 if t < UNITS else K
+            hi = 2 * K if t >= 2 else K
+            codes = work.tile([P, 2 * K], U32, tag="cc", name="cc", align_bytes=64)
+            scales = work.tile([P, 2 * K], U8, tag="sc", name="sc", align_bytes=64)
+            nc.vector.quantize_mx(
+                out=codes[:, lo:hi].bitcast(FP8X4),
+                scales=scales[:, lo:hi],
+                in_=grouped_of(t)[:, PACK * lo : PACK * hi],
+            )
+            quantised[t] = (codes, scales)
+
+        def first_matmul(u):
+            codes, scales = quantised[u]
+            r_t[u] = work.tile([P, PACK, K], F32, tag="rt", name="rt", bufs=4)
+            for t in range(PACK):
+                d_t = bank()
                 nc.tensor.matmul_mx(
-                    out=dz[:, j * P : j * P + P],
-                    lhsT=cc[:, c : c + P].bitcast(FP8X4),
-                    lhsT_scale=sc[:, c : c + P],
-                    rhs=dc[:].bitcast(FP8X4),
-                    rhs_scale=ds[:],
+                    out=d_t[:],
+                    lhsT=w_codes[:, t * P : t * P + P].bitcast(FP8X4),
+                    lhsT_scale=w_scales[:, t * P : t * P + P],
+                    rhs=codes[:, 0:K].bitcast(FP8X4),
+                    rhs_scale=scales[:, 0:K],
                     start=True,
                     stop=True,
                 )
-            st["dz", u] = dz
+                if t == 0:
+                    nc.vector.tensor_scalar(
+                        out=r_t[u][:, t, :],
+                        in0=d_t[:],
+                        scalar1=bias[:, t : t + 1],
+                        scalar2=0.0,
+                        op0=ALU.add,
+                        op1=ALU.max,
+                    )
+                else:
+                    nc.scalar.activation(
+                        out=r_t[u][:, t, :], in_=d_t[:], func=ACT.Relu, bias=bias[:, t : t + 1], scale=1.0
+                    )
 
-        def stage_sq(u):
-            dz = st["dz", u]
-            n2 = work.tile([P, 4], F32, tag="n2", name="n2")
-            for j in range(UT):
-                junk_s = work.tile([P, P], F32, tag="junk_s", name="junk_s", bufs=2)
-                nc.scalar.activation(
-                    out=junk_s[:], in_=dz[:, j * P : j * P + P], func=ACT.Square, accum_out=n2[:, j : j + 1]
+        def regroup_r(u):
+            nc.gpsimd.tensor_scalar(
+                out=grouped_of(u + 2)[:, PACK * K : 2 * PACK * K].rearrange("p (c t) -> p c t", t=PACK),
+                in0=r_t[u][:].rearrange("p t c -> p c t"),
+                scalar1=1.0,
+                scalar2=0.0,
+                op0=ALU.mult,
+                op1=ALU.add,
+            )
+
+        def second_matmul(u):
+            codes, scales = quantised[u + 2]
+            dz_bank[u] = bank()
+            for j in range(UNIT):
+                c = K + j * P
+                nc.tensor.matmul_mx(
+                    out=dz_bank[u][:, j * P : j * P + P],
+                    lhsT=codes[:, c : c + P].bitcast(FP8X4),
+                    lhsT_scale=scales[:, c : c + P],
+                    rhs=d_codes[:].bitcast(FP8X4),
+                    rhs_scale=d_scales[:],
+                    start=True,
+                    stop=True,
                 )
-            nr = work.tile([P, 4], F32, tag="nr", name="nr")
-            nc.scalar.activation(out=nr[:], in_=n2[:], func=ACT.Sqrt)
-            den = work.tile([P, 4], F32, tag="den", name="den")
-            nc.scalar.activation(out=den[:], in_=nr[:], func=ACT.Square, bias=eps[:, 0:1], scale=1.0)
-            st["den", u] = den
 
-        def stage_dot(u):
-            dz = st["dz", u]
-            s = work.tile([P, 4], F32, tag="s", name="s")
-            for j in range(UT):
-                junk_v = work.tile([P, P], F32, tag="junk_v", name="junk_v", bufs=2)
+        def norm(u):
+            sum_sq = work.tile([P, UNIT], F32, tag="n2", name="n2")
+            for j in range(UNIT):
+                squares = work.tile([P, P], F32, tag="junk_s", name="junk_s", bufs=2)
+                nc.scalar.activation(
+                    out=squares[:],
+                    in_=dz_bank[u][:, j * P : j * P + P],
+                    func=ACT.Square,
+                    accum_out=sum_sq[:, j : j + 1],
+                )
+            root = work.tile([P, UNIT], F32, tag="nr", name="nr")
+            nc.scalar.activation(out=root[:], in_=sum_sq[:], func=ACT.Sqrt, bias=tiny[:, 0:1], scale=1.0)
+            denom[u] = work.tile([P, UNIT], F32, tag="den", name="den")
+            nc.scalar.activation(out=denom[u][:], in_=root[:], func=ACT.Square, bias=eps[:, 0:1], scale=1.0)
+
+        def dot_with_x(u):
+            dot[u] = work.tile([P, UNIT], F32, tag="s", name="s")
+            for j in range(UNIT):
+                products = work.tile([P, P], F32, tag="junk_v", name="junk_v", bufs=2)
                 nc.vector.scalar_tensor_tensor(
-                    out=junk_v[:],
-                    in0=dz[:, j * P : j * P + P],
+                    out=products[:],
+                    in0=dz_bank[u][:, j * P : j * P + P],
                     scalar=1.0,
-                    in1=x_of[UT * u + j],
+                    in1=x_tile[UNIT * u + j],
                     op0=ALU.mult,
                     op1=ALU.mult,
-                    accum_out=s[:, j : j + 1],
+                    accum_out=dot[u][:, j : j + 1],
                 )
-            st["s", u] = s
 
-        def stage_p(u):
-            rec = work.tile([P, 4], F32, tag="rec", name="rec")
-            nc.vector.reciprocal(out=rec[:], in_=st["den", u][:])
-            pp = work.tile([P, 4], F32, tag="pp", name="pp")
-            nc.vector.tensor_tensor(out=pp[:], in0=st["s", u][:], in1=rec[:], op=ALU.mult)
-            st["pp", u] = pp
+        def projection_scale(u):
+            inverse = work.tile([P, UNIT], F32, tag="rec", name="rec")
+            nc.vector.reciprocal(out=inverse[:], in_=denom[u][:])
+            scale[u] = work.tile([P, UNIT], F32, tag="pp", name="pp")
+            nc.vector.tensor_tensor(out=scale[u][:], in0=dot[u][:], in1=inverse[:], op=ALU.mult)
 
-        def stage_xp(u):
-            pp = st["pp", u]
-            dz = st["dz", u]
-            xp = work.tile([P, 4, P], F32, tag="xp", name="xp", bufs=4)
-            if eng_of("xp", u) == "s":
-                for j in range(UT):
-                    nc.scalar.activation(
-                        out=xp[:, j, :], in_=dz[:, j * P : j * P + P], func=ACT.Copy, scale=pp[:, j : j + 1]
+        def x_pred(u):
+            xp_sb[u] = work.tile([P, UNIT, P], F32, tag="xp", name="xp", bufs=4)
+            nc.vector.tensor_tensor(
+                out=xp_sb[u][:],
+                in0=dz_bank[u][:].rearrange("p (j c) -> p j c", j=UNIT),
+                in1=scale[u][:].unsqueeze(2).to_broadcast([P, UNIT, P]),
+                op=ALU.mult,
+            )
+
+        def z_pred(u):
+            z_sb[u] = work.tile([P, UNIT, K], F32, tag="zs", name="zs", bufs=4)
+            for j in range(UNIT):
+                r_rows = bank()
+                for t in range(PACK):
+                    nc.tensor.transpose(
+                        r_rows[:, t * P : t * P + P], r_t[u][:, t, j * P : j * P + P], ident[:]
                     )
-            else:
-                nc.vector.tensor_tensor(
-                    out=xp[:],
-                    in0=dz[:].rearrange("p (j c) -> p j c", j=UT),
-                    in1=pp[:].unsqueeze(2).to_broadcast([P, UT, P]),
-                    op=ALU.mult,
-                )
-            st["xp", u] = xp
+                if j == 0 or (j == 1 and u % 2 == 1):
+                    nc.vector.tensor_scalar(
+                        out=z_sb[u][:, j, :], in0=r_rows[:], scalar1=scale[u][:, j : j + 1], scalar2=None, op0=ALU.mult
+                    )
+                else:
+                    nc.scalar.activation(
+                        out=z_sb[u][:, j, :], in_=r_rows[:], func=ACT.Copy, scale=scale[u][:, j : j + 1]
+                    )
+                if u == UNITS - 1:
+                    nc.sync.dma_start(out=z_v[:, UNIT * u + j, :], in_=z_sb[u][:, j, :])
 
-        def stage_e(u, j):
-            rt = st["rt", u]
-            pp = st["pp", u]
-            if j == 0:
-                st["zs", u] = work.tile([P, 4, 512], F32, tag="zs", name="zs", bufs=4)
-            zs = st["zs", u]
-            zb = bank()
-            for ft in range(4):
-                nc.tensor.transpose(zb[:, ft * P : ft * P + P], rt[:, ft, j * P : j * P + P], ident[:])
-            if eng_of("e%d" % j, u) == "s":
-                nc.scalar.activation(out=zs[:, j, :], in_=zb[:], func=ACT.Copy, scale=pp[:, j : j + 1])
-            else:
-                nc.vector.tensor_scalar(
-                    out=zs[:, j, :], in0=zb[:], scalar1=pp[:, j : j + 1], scalar2=None, op0=ALU.mult
-                )
-            if u >= FINE:
-                nc.sync.dma_start(out=z_v[:, UT * u + j, :], in_=zs[:, j, :])
+        def store(u):
+            if u < UNITS - 1:
+                nc.sync.dma_start(out=z_v[:, UNIT * u : UNIT * u + UNIT, :], in_=z_sb[u][:])
+            nc.sync.dma_start(out=xp_v[:, UNIT * u : UNIT * u + UNIT, :], in_=xp_sb[u][:])
 
-        def stage_st(u):
-            if u < FINE:
-                nc.sync.dma_start(out=z_v[:, UT * u : UT * u + UT, :], in_=st["zs", u][:])
-            nc.sync.dma_start(out=xp_v[:, UT * u : UT * u + UT, :], in_=st["xp", u][:])
+        def live(u):
+            return 0 <= u < UNITS
 
-        stages = {
-            "a0": lambda u: stage_a(u, 0),
-            "a1": lambda u: stage_a(u, 1),
-            "Q": stage_q,
-            "b0": lambda u: stage_b(u, 0),
-            "b1": lambda u: stage_b(u, 1),
-            "b2": lambda u: stage_b(u, 2),
-            "b3": lambda u: stage_b(u, 3),
-            "c2": stage_c2,
-            "d": stage_d,
-            "sq": stage_sq,
-            "dot": stage_dot,
-            "p": stage_p,
-            "xp": stage_xp,
-            "e0": lambda u: stage_e(u, 0),
-            "e1": lambda u: stage_e(u, 1),
-            "e2": lambda u: stage_e(u, 2),
-            "e3": lambda u: stage_e(u, 3),
-            "st": stage_st,
-        }
-        max_lag = max(lag for name, lag in ORDER)
-        for t in range(NU + 2 + max_lag):
-            for name, lag in ORDER:
-                limit = NU + 2 if name == "Q" else NU
-                if 0 <= t - lag < limit:
-                    stages[name](t - lag)
+        for t in range(UNITS + 4):
+            if live(t - 4):
+                z_pred(t - 4)
+            if live(t - 2):
+                regroup_r(t - 2)
+            if live(t):
+                transpose_o(t)
+            if live(t - 3):
+                second_matmul(t - 3)
+                norm(t - 3)
+            if live(t - 4):
+                x_pred(t - 4)
+                store(t - 4)
+            if live(t - 1):
+                first_matmul(t - 1)
+            if live(t - 3):
+                dot_with_x(t - 3)
+                projection_scale(t - 3)
+            if t < UNITS + 2:
+                quantise(t)
+            if t == 0:
+                prepare_bias_and_d()

@@ -76,13 +76,16 @@ def tile_originaltemporalsae_pa_t_kernel(tc, o, o_w, o_b, D, x, out_0, out_1):
                     x_tile[X_LOAD * x_loads + l] = x_sb[:, l, :]
                 x_loads += 1
 
-        def transpose_words(grouped32, half, rows0, rows1, on_scalar):
+        def transpose_words(rows0, rows1):
             words = bank()
             for j, rows in enumerate((rows0, rows1)):
                 rows32 = rows.bitcast(F32)
                 for u in range(2):
                     c = (2 * j + u) * P
                     nc.tensor.transpose(words[:, c : c + P], rows32[:, u * P : u * P + P], ident[:])
+            return words
+
+        def copy_words(grouped32, half, words, on_scalar):
             dst = grouped32[:, BANK * half : BANK * (half + 1)].rearrange("q (j r u) -> q j r u", j=2, u=2)
             src = words[:].rearrange("q (j u r) -> q j r u", j=2, u=2)
             if on_scalar:
@@ -91,8 +94,9 @@ def tile_originaltemporalsae_pa_t_kernel(tc, o, o_w, o_b, D, x, out_0, out_1):
                 nc.vector.tensor_copy(out=dst, in_=src)
 
         w_grouped = const.tile([P, PACK * K], BF16, name="wg", align_bytes=64)
-        transpose_words(w_grouped[:].bitcast(F32), 0, w_sb[:, 0, :], w_sb[:, 1, :], False)
-        transpose_words(w_grouped[:].bitcast(F32), 1, w_sb[:, 2, :], w_sb[:, 3, :], True)
+        for half in range(2):
+            words = transpose_words(w_sb[:, 2 * half, :], w_sb[:, 2 * half + 1, :])
+            copy_words(w_grouped[:].bitcast(F32), half, words, half == 1)
         w_codes = const.tile([P, K], U32, name="wc", align_bytes=64)
         w_scales = const.tile([P, K], U8, name="ws", align_bytes=64)
         nc.vector.quantize_mx(out=w_codes[:].bitcast(FP8X4), scales=w_scales[:], in_=w_grouped[:])
@@ -113,69 +117,81 @@ def tile_originaltemporalsae_pa_t_kernel(tc, o, o_w, o_b, D, x, out_0, out_1):
                 out=d_codes[:].bitcast(FP8X4), scales=d_scales[:], in_=d_grouped[:].rearrange("p j t -> p (j t)")
             )
 
-        grouped = {}
-        quantised = {}
+        o_grouped = {}
+        r_grouped = {}
+        o_quantised = {}
+        r_quantised = {}
+        o_bank = {}
+        d_bank = {}
         r_t = {}
+        r_bank = {}
+        dz = {}
         dz_bank = {}
+        sum_sq = {}
+        root = {}
         denom = {}
+        inverse = {}
         dot = {}
         scale = {}
         z_sb = {}
         xp_sb = {}
 
-        def grouped_of(t):
-            if t not in grouped:
-                grouped[t] = work.tile([P, 2 * PACK * K], BF16, tag="gg", name="gg", bufs=1, align_bytes=64)
-            return grouped[t]
+        def o_grouped_of(u):
+            if u not in o_grouped:
+                o_grouped[u] = work.tile([P, PACK * K], BF16, tag="go", name="go", bufs=2, align_bytes=64)
+            return o_grouped[u]
 
-        def transpose_o(u):
-            grouped32 = grouped_of(u)[:, 0 : PACK * K].bitcast(F32)
-            transpose_words(grouped32, 0, o_tile[UNIT * u], o_tile[UNIT * u + 1], True)
-            transpose_words(grouped32, 1, o_tile[UNIT * u + 2], o_tile[UNIT * u + 3], False)
+        def r_grouped_of(u):
+            if u not in r_grouped:
+                r_grouped[u] = work.tile([P, PACK * K], BF16, tag="gr", name="gr", bufs=1, align_bytes=64)
+            return r_grouped[u]
 
-        def quantise(t):
-            lo = 0 if t < UNITS else K
-            hi = 2 * K if t >= 2 else K
-            codes = work.tile([P, 2 * K], U32, tag="cc", name="cc", align_bytes=64)
-            scales = work.tile([P, 2 * K], U8, tag="sc", name="sc", align_bytes=64)
-            nc.vector.quantize_mx(
-                out=codes[:, lo:hi].bitcast(FP8X4),
-                scales=scales[:, lo:hi],
-                in_=grouped_of(t)[:, PACK * lo : PACK * hi],
+        def transpose_o(u, half):
+            row_tile = UNIT * u + 2 * half
+            o_bank[u, half] = transpose_words(o_tile[row_tile], o_tile[row_tile + 1])
+
+        def copy_o(u, half, on_scalar):
+            copy_words(o_grouped_of(u)[:].bitcast(F32), half, o_bank[u, half], on_scalar)
+
+        def quantise(grouped):
+            codes = work.tile([P, K], U32, tag="cc", name="cc", bufs=5, align_bytes=64)
+            scales = work.tile([P, K], U8, tag="sc", name="sc", bufs=5, align_bytes=64)
+            nc.vector.quantize_mx(out=codes[:].bitcast(FP8X4), scales=scales[:], in_=grouped[:])
+            return codes, scales
+
+        def first_matmul(u, t):
+            codes, scales = o_quantised[u]
+            d_bank[u, t] = bank()
+            nc.tensor.matmul_mx(
+                out=d_bank[u, t][:],
+                lhsT=w_codes[:, t * P : t * P + P].bitcast(FP8X4),
+                lhsT_scale=w_scales[:, t * P : t * P + P],
+                rhs=codes[:].bitcast(FP8X4),
+                rhs_scale=scales[:],
+                start=True,
+                stop=True,
             )
-            quantised[t] = (codes, scales)
 
-        def first_matmul(u):
-            codes, scales = quantised[u]
-            r_t[u] = work.tile([P, PACK, K], F32, tag="rt", name="rt", bufs=4)
-            for t in range(PACK):
-                d_t = bank()
-                nc.tensor.matmul_mx(
-                    out=d_t[:],
-                    lhsT=w_codes[:, t * P : t * P + P].bitcast(FP8X4),
-                    lhsT_scale=w_scales[:, t * P : t * P + P],
-                    rhs=codes[:, 0:K].bitcast(FP8X4),
-                    rhs_scale=scales[:, 0:K],
-                    start=True,
-                    stop=True,
+        def bias_relu(u, t, on_scalar):
+            if u not in r_t:
+                r_t[u] = work.tile([P, PACK, K], F32, tag="rt", name="rt", bufs=4)
+            if not on_scalar:
+                nc.vector.tensor_scalar(
+                    out=r_t[u][:, t, :],
+                    in0=d_bank[u, t][:],
+                    scalar1=bias[:, t : t + 1],
+                    scalar2=0.0,
+                    op0=ALU.add,
+                    op1=ALU.max,
                 )
-                if t == 0:
-                    nc.vector.tensor_scalar(
-                        out=r_t[u][:, t, :],
-                        in0=d_t[:],
-                        scalar1=bias[:, t : t + 1],
-                        scalar2=0.0,
-                        op0=ALU.add,
-                        op1=ALU.max,
-                    )
-                else:
-                    nc.scalar.activation(
-                        out=r_t[u][:, t, :], in_=d_t[:], func=ACT.Relu, bias=bias[:, t : t + 1], scale=1.0
-                    )
+            else:
+                nc.scalar.activation(
+                    out=r_t[u][:, t, :], in_=d_bank[u, t][:], func=ACT.Relu, bias=bias[:, t : t + 1], scale=1.0
+                )
 
         def regroup_r(u):
             nc.gpsimd.tensor_scalar(
-                out=grouped_of(u + 2)[:, PACK * K : 2 * PACK * K].rearrange("p (c t) -> p c t", t=PACK),
+                out=r_grouped_of(u)[:].rearrange("p (c t) -> p c t", t=PACK),
                 in0=r_t[u][:].rearrange("p t c -> p c t"),
                 scalar1=1.0,
                 scalar2=0.0,
@@ -183,13 +199,14 @@ def tile_originaltemporalsae_pa_t_kernel(tc, o, o_w, o_b, D, x, out_0, out_1):
                 op1=ALU.add,
             )
 
-        def second_matmul(u):
-            codes, scales = quantised[u + 2]
-            dz_bank[u] = bank()
-            for j in range(UNIT):
-                c = K + j * P
+        def second_matmul(u, tiles):
+            codes, scales = r_quantised[u]
+            out = bank()
+            for i, j in enumerate(tiles):
+                c = j * P
+                dz[u, j] = out[:, i * P : i * P + P]
                 nc.tensor.matmul_mx(
-                    out=dz_bank[u][:, j * P : j * P + P],
+                    out=dz[u, j],
                     lhsT=codes[:, c : c + P].bitcast(FP8X4),
                     lhsT_scale=scales[:, c : c + P],
                     rhs=d_codes[:].bitcast(FP8X4),
@@ -197,69 +214,80 @@ def tile_originaltemporalsae_pa_t_kernel(tc, o, o_w, o_b, D, x, out_0, out_1):
                     start=True,
                     stop=True,
                 )
+            dz_bank[u, tiles[0]] = out
 
-        def norm(u):
-            sum_sq = work.tile([P, UNIT], F32, tag="n2", name="n2")
-            for j in range(UNIT):
-                squares = work.tile([P, P], F32, tag="junk_s", name="junk_s", bufs=2)
-                nc.scalar.activation(
-                    out=squares[:],
-                    in_=dz_bank[u][:, j * P : j * P + P],
-                    func=ACT.Square,
-                    accum_out=sum_sq[:, j : j + 1],
-                )
-            root = work.tile([P, UNIT], F32, tag="nr", name="nr")
-            nc.scalar.activation(out=root[:], in_=sum_sq[:], func=ACT.Sqrt, bias=tiny[:, 0:1], scale=1.0)
+        def square_sum(u, j):
+            if u not in sum_sq:
+                sum_sq[u] = work.tile([P, UNIT], F32, tag="n2", name="n2")
+            squares = work.tile([P, P], F32, tag="junk_s", name="junk_s", bufs=2)
+            nc.scalar.activation(
+                out=squares[:], in_=dz[u, j], func=ACT.Square, accum_out=sum_sq[u][:, j : j + 1]
+            )
+
+        def take_root(u):
+            root[u] = work.tile([P, UNIT], F32, tag="nr", name="nr")
+            nc.scalar.activation(out=root[u][:], in_=sum_sq[u][:], func=ACT.Sqrt, bias=tiny[:, 0:1], scale=1.0)
+
+        def denominator(u):
             denom[u] = work.tile([P, UNIT], F32, tag="den", name="den")
-            nc.scalar.activation(out=denom[u][:], in_=root[:], func=ACT.Square, bias=eps[:, 0:1], scale=1.0)
+            nc.scalar.activation(out=denom[u][:], in_=root[u][:], func=ACT.Square, bias=eps[:, 0:1], scale=1.0)
 
-        def dot_with_x(u):
-            dot[u] = work.tile([P, UNIT], F32, tag="s", name="s")
-            for j in range(UNIT):
-                products = work.tile([P, P], F32, tag="junk_v", name="junk_v", bufs=2)
-                nc.vector.scalar_tensor_tensor(
-                    out=products[:],
-                    in0=dz_bank[u][:, j * P : j * P + P],
-                    scalar=1.0,
-                    in1=x_tile[UNIT * u + j],
-                    op0=ALU.mult,
-                    op1=ALU.mult,
-                    accum_out=dot[u][:, j : j + 1],
-                )
+        def dot_with_x(u, j):
+            if u not in dot:
+                dot[u] = work.tile([P, UNIT], F32, tag="s", name="s")
+            products = work.tile([P, P], F32, tag="junk_v", name="junk_v", bufs=2)
+            nc.vector.scalar_tensor_tensor(
+                out=products[:],
+                in0=dz[u, j],
+                scalar=1.0,
+                in1=x_tile[UNIT * u + j],
+                op0=ALU.mult,
+                op1=ALU.mult,
+                accum_out=dot[u][:, j : j + 1],
+            )
+
+        def invert(u):
+            inverse[u] = work.tile([P, UNIT], F32, tag="rec", name="rec")
+            nc.vector.reciprocal(out=inverse[u][:], in_=denom[u][:])
 
         def projection_scale(u):
-            inverse = work.tile([P, UNIT], F32, tag="rec", name="rec")
-            nc.vector.reciprocal(out=inverse[:], in_=denom[u][:])
             scale[u] = work.tile([P, UNIT], F32, tag="pp", name="pp")
-            nc.vector.tensor_tensor(out=scale[u][:], in0=dot[u][:], in1=inverse[:], op=ALU.mult)
+            nc.vector.tensor_tensor(out=scale[u][:], in0=dot[u][:], in1=inverse[u][:], op=ALU.mult)
 
-        def x_pred(u):
-            xp_sb[u] = work.tile([P, UNIT, P], F32, tag="xp", name="xp", bufs=4)
+        def x_pred(u, j, n):
+            if u not in xp_sb:
+                xp_sb[u] = work.tile([P, UNIT, P], F32, tag="xp", name="xp", bufs=4)
             nc.vector.tensor_tensor(
-                out=xp_sb[u][:],
-                in0=dz_bank[u][:].rearrange("p (j c) -> p j c", j=UNIT),
-                in1=scale[u][:].unsqueeze(2).to_broadcast([P, UNIT, P]),
+                out=xp_sb[u][:, j : j + n, :],
+                in0=dz_bank[u, j][:, 0 : n * P].rearrange("p (j c) -> p j c", j=n),
+                in1=scale[u][:, j : j + n].unsqueeze(2).to_broadcast([P, n, P]),
                 op=ALU.mult,
             )
 
-        def z_pred(u):
-            z_sb[u] = work.tile([P, UNIT, K], F32, tag="zs", name="zs", bufs=4)
-            for j in range(UNIT):
-                r_rows = bank()
-                for t in range(PACK):
-                    nc.tensor.transpose(
-                        r_rows[:, t * P : t * P + P], r_t[u][:, t, j * P : j * P + P], ident[:]
-                    )
-                if j == 0 or (j == 1 and u % 2 == 1):
-                    nc.vector.tensor_scalar(
-                        out=z_sb[u][:, j, :], in0=r_rows[:], scalar1=scale[u][:, j : j + 1], scalar2=None, op0=ALU.mult
-                    )
-                else:
-                    nc.scalar.activation(
-                        out=z_sb[u][:, j, :], in_=r_rows[:], func=ACT.Copy, scale=scale[u][:, j : j + 1]
-                    )
-                if u == UNITS - 1:
-                    nc.sync.dma_start(out=z_v[:, UNIT * u + j, :], in_=z_sb[u][:, j, :])
+        def x_pred_scalar(u, j):
+            if u not in xp_sb:
+                xp_sb[u] = work.tile([P, UNIT, P], F32, tag="xp", name="xp", bufs=4)
+            nc.scalar.activation(out=xp_sb[u][:, j, :], in_=dz[u, j], func=ACT.Copy, scale=scale[u][:, j : j + 1])
+
+        def transpose_r(u, j):
+            r_bank[u, j] = bank()
+            for t in range(PACK):
+                nc.tensor.transpose(
+                    r_bank[u, j][:, t * P : t * P + P], r_t[u][:, t, j * P : j * P + P], ident[:]
+                )
+
+        def z_pred(u, j, on_scalar):
+            if u not in z_sb:
+                z_sb[u] = work.tile([P, UNIT, K], F32, tag="zs", name="zs", bufs=4)
+            p = scale[u][:, j : j + 1]
+            if on_scalar:
+                nc.scalar.activation(out=z_sb[u][:, j, :], in_=r_bank[u, j][:], func=ACT.Copy, scale=p)
+            else:
+                nc.vector.tensor_scalar(
+                    out=z_sb[u][:, j, :], in0=r_bank[u, j][:], scalar1=p, scalar2=None, op0=ALU.mult
+                )
+            if u == UNITS - 1:
+                nc.sync.dma_start(out=z_v[:, UNIT * u + j, :], in_=z_sb[u][:, j, :])
 
         def store(u):
             if u < UNITS - 1:
@@ -270,24 +298,66 @@ def tile_originaltemporalsae_pa_t_kernel(tc, o, o_w, o_b, D, x, out_0, out_1):
             return 0 <= u < UNITS
 
         for t in range(UNITS + 4):
-            if live(t - 4):
-                z_pred(t - 4)
-            if live(t - 2):
-                regroup_r(t - 2)
-            if live(t):
-                transpose_o(t)
-            if live(t - 3):
-                second_matmul(t - 3)
-                norm(t - 3)
-            if live(t - 4):
-                x_pred(t - 4)
-                store(t - 4)
-            if live(t - 1):
-                first_matmul(t - 1)
-            if live(t - 3):
-                dot_with_x(t - 3)
-                projection_scale(t - 3)
-            if t < UNITS + 2:
-                quantise(t)
+            o_, f, c, s, z = (t - i if live(t - i) else None for i in range(5))
+            if z is not None:
+                vz = (0, 2)
+                sz = [j for j in range(4) if j not in vz]
+            if o_ is not None:
+                transpose_o(o_, 0)
+            if z is not None:
+                for j in range(4):
+                    transpose_r(z, j)
+                z_pred(z, sz[0], True)
+            if o_ is not None:
+                transpose_o(o_, 1)
+                copy_o(o_, 0, True)
+            if z is not None:
+                for j in vz:
+                    z_pred(z, j, False)
+                for j in sz[1:]:
+                    z_pred(z, j, True)
+            if s is not None:
+                second_matmul(s, (0, 1))
+                second_matmul(s, (2, 3))
+                for j in range(4):
+                    square_sum(s, j)
+            if z is not None:
+                x_pred(z, 0, 2)
+            if o_ is not None:
+                copy_o(o_, 1, False)
+            if z is not None:
+                x_pred(z, 2, 2)
+            if f is not None:
+                for k in range(4):
+                    first_matmul(f, k)
+            if s is not None:
+                take_root(s)
+                denominator(s)
+            if f is not None:
+                bias_relu(f, 1, True)
+            if s is not None:
+                for j in range(4):
+                    dot_with_x(s, j)
+            if s is not None:
+                invert(s)
+            if f is not None:
+                bias_relu(f, 0, False)
+            if s is not None:
+                projection_scale(s)
+            if z is not None:
+                store(z)
+            def qo():
+                if o_ is not None:
+                    o_quantised[o_] = quantise(o_grouped_of(o_))
+            def qr():
+                if c is not None:
+                    r_quantised[c] = quantise(r_grouped_of(c))
+            if c is not None:
+                regroup_r(c)
+            qo()
+            qr()
+            if f is not None:
+                bias_relu(f, 2, True)
+                bias_relu(f, 3, True)
             if t == 0:
                 prepare_bias_and_d()

@@ -23,6 +23,8 @@ TINY = 1e-30
 FLOPS = 2 * 8192 * K * K + 2 * 8192 * K * P
 
 O_LOADS = [2, 2, 4, 8, 8, 8, 8, 8, 8, 8]
+WARM_UP = 5
+VECTOR_ROWS = 352
 X_LOAD = 16
 
 
@@ -52,6 +54,11 @@ def tile_originaltemporalsae_pa_t_kernel(tc, o, o_w, o_b, D, x, out_0, out_1):
         make_identity(nc, ident[:])
         bias_rows = const.tile([P, P], BF16, name="bz")
         nc.vector.memset(bias_rows[:], 0.0)
+
+        zeros = const.tile([P, BANK], BF16, name="zeros")
+        nc.vector.memset(zeros[:], 0.0)
+        for i in range(WARM_UP):
+            nc.tensor.matmul(bank()[:], lhsT=zeros[:, 0:P], rhs=zeros[:], start=True, stop=True)
 
         w_sb = const.tile([P, PACK, K], BF16, name="w_sb")
         nc.sync.dma_start(out=w_sb[:], in_=o_w.rearrange("(a p) k -> p a k", p=P))
@@ -93,6 +100,23 @@ def tile_originaltemporalsae_pa_t_kernel(tc, o, o_w, o_b, D, x, out_0, out_1):
             else:
                 nc.vector.tensor_copy(out=dst, in_=src)
 
+        bias_rows32 = const.tile([P, P], F32, name="bzf")
+        bias = const.tile([P, PACK], F32, name="b_sb")
+        d_grouped = const.tile([P, P, PACK], BF16, name="dg", align_bytes=64)
+        d_codes = const.tile([P, P], U32, name="dc", align_bytes=64)
+        d_scales = const.tile([P, P], U8, name="ds", align_bytes=64)
+
+        def prepare_bias():
+            bias_t = bank()
+            nc.tensor.transpose(bias_t[:, 0:P], bias_rows32[:], ident[:])
+            nc.vector.tensor_copy(out=bias[:], in_=bias_t[:, 0:PACK])
+
+        def prepare_d():
+            nc.vector.tensor_copy(out=d_grouped[:], in_=d_sb[:].rearrange("p t j -> p j t"))
+            nc.vector.quantize_mx(
+                out=d_codes[:].bitcast(FP8X4), scales=d_scales[:], in_=d_grouped[:].rearrange("p j t -> p (j t)")
+            )
+
         w_grouped = const.tile([P, PACK * K], BF16, name="wg", align_bytes=64)
         for half in range(2):
             words = transpose_words(w_sb[:, 2 * half, :], w_sb[:, 2 * half + 1, :])
@@ -100,22 +124,6 @@ def tile_originaltemporalsae_pa_t_kernel(tc, o, o_w, o_b, D, x, out_0, out_1):
         w_codes = const.tile([P, K], U32, name="wc", align_bytes=64)
         w_scales = const.tile([P, K], U8, name="ws", align_bytes=64)
         nc.vector.quantize_mx(out=w_codes[:].bitcast(FP8X4), scales=w_scales[:], in_=w_grouped[:])
-
-        bias_rows32 = const.tile([P, P], F32, name="bzf")
-        bias = const.tile([P, PACK], F32, name="b_sb")
-        d_grouped = const.tile([P, P, PACK], BF16, name="dg", align_bytes=64)
-        d_codes = const.tile([P, P], U32, name="dc", align_bytes=64)
-        d_scales = const.tile([P, P], U8, name="ds", align_bytes=64)
-
-        def prepare_bias_and_d():
-            nc.vector.tensor_copy(out=bias_rows32[:], in_=bias_rows[:])
-            bias_t = bank()
-            nc.tensor.transpose(bias_t[:, 0:P], bias_rows32[:], ident[:])
-            nc.vector.tensor_copy(out=bias[:], in_=bias_t[:, 0:PACK])
-            nc.vector.tensor_copy(out=d_grouped[:], in_=d_sb[:].rearrange("p t j -> p j t"))
-            nc.vector.quantize_mx(
-                out=d_codes[:].bitcast(FP8X4), scales=d_scales[:], in_=d_grouped[:].rearrange("p j t -> p (j t)")
-            )
 
         o_grouped = {}
         r_grouped = {}
@@ -190,14 +198,14 @@ def tile_originaltemporalsae_pa_t_kernel(tc, o, o_w, o_b, D, x, out_0, out_1):
                 )
 
         def regroup_r(u):
-            nc.gpsimd.tensor_scalar(
-                out=r_grouped_of(u)[:].rearrange("p (c t) -> p c t", t=PACK),
-                in0=r_t[u][:].rearrange("p t c -> p c t"),
-                scalar1=1.0,
-                scalar2=0.0,
-                op0=ALU.mult,
-                op1=ALU.add,
-            )
+            dst = r_grouped_of(u)[:].rearrange("p (c t) -> p c t", t=PACK)
+            src = r_t[u][:].rearrange("p t c -> p c t")
+            if u == 0:
+                a = VECTOR_ROWS
+                nc.vector.tensor_copy(out=dst[:, 0:a, :], in_=src[:, 0:a, :])
+                nc.scalar.copy(out=dst[:, a:, :], in_=src[:, a:, :])
+            else:
+                nc.gpsimd.tensor_scalar(out=dst, in0=src, scalar1=1.0, scalar2=0.0, op0=ALU.mult, op1=ALU.add)
 
         def second_matmul(u, tiles):
             codes, scales = r_quantised[u]
@@ -298,66 +306,62 @@ def tile_originaltemporalsae_pa_t_kernel(tc, o, o_w, o_b, D, x, out_0, out_1):
             return 0 <= u < UNITS
 
         for t in range(UNITS + 4):
-            o_, f, c, s, z = (t - i if live(t - i) else None for i in range(5))
-            if z is not None:
-                vz = (0, 2)
-                sz = [j for j in range(4) if j not in vz]
-            if o_ is not None:
-                transpose_o(o_, 0)
-            if z is not None:
-                for j in range(4):
-                    transpose_r(z, j)
-                z_pred(z, sz[0], True)
-            if o_ is not None:
-                transpose_o(o_, 1)
-                copy_o(o_, 0, True)
-            if z is not None:
-                for j in vz:
-                    z_pred(z, j, False)
-                for j in sz[1:]:
-                    z_pred(z, j, True)
-            if s is not None:
-                second_matmul(s, (0, 1))
-                second_matmul(s, (2, 3))
-                for j in range(4):
-                    square_sum(s, j)
-            if z is not None:
-                x_pred(z, 0, 2)
-            if o_ is not None:
-                copy_o(o_, 1, False)
-            if z is not None:
-                x_pred(z, 2, 2)
-            if f is not None:
-                for k in range(4):
-                    first_matmul(f, k)
-            if s is not None:
-                take_root(s)
-                denominator(s)
-            if f is not None:
-                bias_relu(f, 1, True)
-            if s is not None:
-                for j in range(4):
-                    dot_with_x(s, j)
-            if s is not None:
-                invert(s)
-            if f is not None:
-                bias_relu(f, 0, False)
-            if s is not None:
-                projection_scale(s)
-            if z is not None:
-                store(z)
-            def qo():
-                if o_ is not None:
-                    o_quantised[o_] = quantise(o_grouped_of(o_))
-            def qr():
-                if c is not None:
-                    r_quantised[c] = quantise(r_grouped_of(c))
-            if c is not None:
-                regroup_r(c)
-            qo()
-            qr()
-            if f is not None:
-                bias_relu(f, 2, True)
-                bias_relu(f, 3, True)
+            new, first, cast, second, last = (t - i if live(t - i) else None for i in range(5))
+            if new is not None:
+                transpose_o(new, 0)
+            if last is not None:
+                for j in range(UNIT):
+                    transpose_r(last, j)
+                z_pred(last, 1, True)
+            if new is not None:
+                transpose_o(new, 1)
+                copy_o(new, 0, True)
+            if t == 1:
+                prepare_bias()
+            if last is not None:
+                z_pred(last, 0, False)
+                z_pred(last, 2, False)
+                z_pred(last, 3, True)
+            if second is not None:
+                second_matmul(second, (0, 1))
+                second_matmul(second, (2, 3))
+                for j in range(UNIT):
+                    square_sum(second, j)
+            if last is not None:
+                x_pred(last, 0, 2)
+            if new is not None:
+                copy_o(new, 1, False)
+            if t == 1:
+                prepare_d()
+            if first is not None:
+                for k in range(PACK):
+                    first_matmul(first, k)
+            if last is not None:
+                x_pred_scalar(last, 2)
+            if second is not None:
+                take_root(second)
+            if last is not None:
+                x_pred_scalar(last, 3)
+                store(last)
+            if second is not None:
+                denominator(second)
+            if first is not None:
+                bias_relu(first, 1, True)
+            if second is not None:
+                for j in range(UNIT):
+                    dot_with_x(second, j)
+                invert(second)
+            if first is not None:
+                bias_relu(first, 0, False)
+            if second is not None:
+                projection_scale(second)
+            if cast is not None:
+                regroup_r(cast)
+                r_quantised[cast] = quantise(r_grouped_of(cast))
+            if new is not None:
+                o_quantised[new] = quantise(o_grouped_of(new))
             if t == 0:
-                prepare_bias_and_d()
+                nc.vector.tensor_copy(out=bias_rows32[:], in_=bias_rows[:])
+            if first is not None:
+                bias_relu(first, 2, True)
+                bias_relu(first, 3, True)

@@ -23,7 +23,7 @@ TINY = 1e-30
 FLOPS = 2 * 8192 * K * K + 2 * 8192 * K * P
 
 O_LOADS = [2, 2, 4, 8, 8, 8, 8, 8, 8, 8]
-WARM_UP = 5
+WARM_UP = 4
 VECTOR_ROWS = 352
 X_LOAD = 16
 
@@ -44,6 +44,10 @@ def tile_originaltemporalsae_pa_t_kernel(tc, o, o_w, o_b, D, x, out_0, out_1):
         def bank():
             return psum.tile([P, BANK], F32, tag="bank", name="bank")
 
+        zeros = const.tile([P, BANK], BF16, name="zeros")
+        nc.vector.memset(zeros[:], 0.0)
+        bias_rows = const.tile([P, P], BF16, name="bz")
+        nc.vector.memset(bias_rows[:], 0.0)
         eps = const.tile([P, 1], F32, name="eps")
         nc.vector.memset(eps[:], EPS)
         tiny = const.tile([P, 1], F32, name="tiny")
@@ -52,19 +56,12 @@ def tile_originaltemporalsae_pa_t_kernel(tc, o, o_w, o_b, D, x, out_0, out_1):
         nc.scalar.activation(out=warm[:], in_=eps[:], func=ACT.Sqrt)
         ident = const.tile([P, P], F32, name="ident")
         make_identity(nc, ident[:])
-        bias_rows = const.tile([P, P], BF16, name="bz")
-        nc.vector.memset(bias_rows[:], 0.0)
-
-        zeros = const.tile([P, BANK], BF16, name="zeros")
-        nc.vector.memset(zeros[:], 0.0)
         for i in range(WARM_UP):
             nc.tensor.matmul(bank()[:], lhsT=zeros[:, 0:P], rhs=zeros[:], start=True, stop=True)
 
         w_sb = const.tile([P, PACK, K], BF16, name="w_sb")
         nc.sync.dma_start(out=w_sb[:], in_=o_w.rearrange("(a p) k -> p a k", p=P))
-        nc.scalar.dma_start(out=bias_rows[0:PACK, :], in_=o_b.rearrange("(t p) -> t p", p=P))
         d_sb = const.tile([P, PACK, P], BF16, name="d_sb")
-        nc.scalar.dma_start(out=d_sb[:], in_=D.rearrange("(t p) j -> p t j", p=P))
 
         o_tile = {}
         x_tile = {}
@@ -76,6 +73,10 @@ def tile_originaltemporalsae_pa_t_kernel(tc, o, o_w, o_b, D, x, out_0, out_1):
             for l in range(n):
                 o_tile[first + l] = o_sb[:, l, :]
             first += n
+            if g == 1:
+                nc.sync.dma_start(out=bias_rows[0:PACK, :], in_=o_b.rearrange("(t p) -> t p", p=P))
+            if g == 2:
+                nc.sync.dma_start(out=d_sb[:], in_=D.rearrange("(t p) j -> p t j", p=P))
             if g >= 2 and x_loads < TILES // X_LOAD:
                 x_sb = const.tile([P, X_LOAD, P], BF16, name="xch%d" % x_loads)
                 nc.sync.dma_start(out=x_sb[:], in_=x_v[:, X_LOAD * x_loads : X_LOAD * (x_loads + 1), :])
@@ -121,6 +122,7 @@ def tile_originaltemporalsae_pa_t_kernel(tc, o, o_w, o_b, D, x, out_0, out_1):
         for half in range(2):
             words = transpose_words(w_sb[:, 2 * half, :], w_sb[:, 2 * half + 1, :])
             copy_words(w_grouped[:].bitcast(F32), half, words, half == 1)
+        nc.vector.tensor_copy(out=bias_rows32[:], in_=bias_rows[:])
         w_codes = const.tile([P, K], U32, name="wc", align_bytes=64)
         w_scales = const.tile([P, K], U8, name="ws", align_bytes=64)
         nc.vector.quantize_mx(out=w_codes[:].bitcast(FP8X4), scales=w_scales[:], in_=w_grouped[:])
@@ -307,16 +309,27 @@ def tile_originaltemporalsae_pa_t_kernel(tc, o, o_w, o_b, D, x, out_0, out_1):
 
         for t in range(UNITS + 4):
             new, first, cast, second, last = (t - i if live(t - i) else None for i in range(5))
+            if cast == 0:
+                regroup_r(cast)
+                r_quantised[cast] = quantise(r_grouped_of(cast))
             if new is not None:
                 transpose_o(new, 0)
             if last is not None:
-                for j in range(UNIT):
+                for j in range(0):
+                    transpose_r(last, j)
+            if cast is not None and cast > 0:
+                for k in (2, 3):
+                    first_matmul(cast, k)
+                bias_relu(cast, 2, True)
+                bias_relu(cast, 3, True)
+            if last is not None:
+                for j in range(0, UNIT):
                     transpose_r(last, j)
                 z_pred(last, 1, True)
             if new is not None:
                 transpose_o(new, 1)
                 copy_o(new, 0, True)
-            if t == 1:
+            if t == 0:
                 prepare_bias()
             if last is not None:
                 z_pred(last, 0, False)
@@ -334,7 +347,7 @@ def tile_originaltemporalsae_pa_t_kernel(tc, o, o_w, o_b, D, x, out_0, out_1):
             if t == 1:
                 prepare_d()
             if first is not None:
-                for k in range(PACK):
+                for k in range(PACK if first == 0 else 2):
                     first_matmul(first, k)
             if last is not None:
                 x_pred_scalar(last, 2)
@@ -355,13 +368,11 @@ def tile_originaltemporalsae_pa_t_kernel(tc, o, o_w, o_b, D, x, out_0, out_1):
                 bias_relu(first, 0, False)
             if second is not None:
                 projection_scale(second)
-            if cast is not None:
+            if cast is not None and cast > 0:
                 regroup_r(cast)
                 r_quantised[cast] = quantise(r_grouped_of(cast))
-            if new is not None:
-                o_quantised[new] = quantise(o_grouped_of(new))
-            if t == 0:
-                nc.vector.tensor_copy(out=bias_rows32[:], in_=bias_rows[:])
-            if first is not None:
+            if first == 0:
                 bias_relu(first, 2, True)
                 bias_relu(first, 3, True)
+            if new is not None:
+                o_quantised[new] = quantise(o_grouped_of(new))

@@ -273,11 +273,15 @@ def tile_originaltemporalsae_pa_t_kernel(tc, o, o_w, o_b, D, x, out_0, out_1):
                 in1=scale[u][:, j : j + n].unsqueeze(2).to_broadcast([P, n, P]),
                 op=ALU.mult,
             )
+            if u >= UNITS - 2:
+                nc.sync.dma_start(out=xp_v[:, UNIT * u + j : UNIT * u + j + n, :], in_=xp_sb[u][:, j : j + n, :])
 
         def x_pred_scalar(u, j):
             if u not in xp_sb:
                 xp_sb[u] = work.tile([P, UNIT, P], F32, tag="xp", name="xp", bufs=4)
             nc.scalar.activation(out=xp_sb[u][:, j, :], in_=dz[u, j], func=ACT.Copy, scale=scale[u][:, j : j + 1])
+            if u >= UNITS - 2:
+                nc.sync.dma_start(out=xp_v[:, UNIT * u + j, :], in_=xp_sb[u][:, j, :])
 
         def transpose_r(u, j):
             r_bank[u, j] = bank()
@@ -296,59 +300,68 @@ def tile_originaltemporalsae_pa_t_kernel(tc, o, o_w, o_b, D, x, out_0, out_1):
                 nc.vector.tensor_scalar(
                     out=z_sb[u][:, j, :], in0=r_bank[u, j][:], scalar1=p, scalar2=None, op0=ALU.mult
                 )
-            if u == UNITS - 1:
+            if u >= UNITS - 2:
                 nc.sync.dma_start(out=z_v[:, UNIT * u + j, :], in_=z_sb[u][:, j, :])
 
         def store(u):
-            if u < UNITS - 1:
+            if u < UNITS - 2:
                 nc.sync.dma_start(out=z_v[:, UNIT * u : UNIT * u + UNIT, :], in_=z_sb[u][:])
-            nc.sync.dma_start(out=xp_v[:, UNIT * u : UNIT * u + UNIT, :], in_=xp_sb[u][:])
+                nc.sync.dma_start(out=xp_v[:, UNIT * u : UNIT * u + UNIT, :], in_=xp_sb[u][:])
 
         def live(u):
             return 0 <= u < UNITS
 
         for t in range(UNITS + 4):
+            LATE = (2, 3)
             new, first, cast, second, last = (t - i if live(t - i) else None for i in range(5))
             if cast == 0:
                 regroup_r(cast)
                 r_quantised[cast] = quantise(r_grouped_of(cast))
             if new is not None:
                 transpose_o(new, 0)
-            if last is not None:
-                for j in range(0):
-                    transpose_r(last, j)
             if cast is not None and cast > 0:
-                for k in (2, 3):
+                for k in LATE:
                     first_matmul(cast, k)
-                bias_relu(cast, 2, True)
-                bias_relu(cast, 3, True)
             if last is not None:
-                for j in range(0, UNIT):
-                    transpose_r(last, j)
-                z_pred(last, 1, True)
+                transpose_r(last, 0)
+            if last is not None:
+                transpose_r(last, 1)
+            if last is not None:
+                transpose_r(last, 2)
+            if last is not None:
+                transpose_r(last, 3)
             if new is not None:
                 transpose_o(new, 1)
-                copy_o(new, 0, True)
+            if second is not None:
+                second_matmul(second, (0, 1))
+            if second is not None:
+                second_matmul(second, (2, 3))
+            if first is not None:
+                for k in (1, 0, 2, 3):
+                    if first == 0 or k not in LATE:
+                        first_matmul(first, k)
             if t == 0:
                 prepare_bias()
+            if cast is not None and cast > 0:
+                for k in LATE:
+                    bias_relu(cast, k, True)
+            if last is not None:
+                z_pred(last, 1, True)
+            if new is not None:
+                copy_o(new, 0, True)
             if last is not None:
                 z_pred(last, 0, False)
                 z_pred(last, 2, False)
                 z_pred(last, 3, True)
             if second is not None:
-                second_matmul(second, (0, 1))
-                second_matmul(second, (2, 3))
                 for j in range(UNIT):
                     square_sum(second, j)
-            if last is not None:
-                x_pred(last, 0, 2)
             if new is not None:
                 copy_o(new, 1, False)
+            if last is not None:
+                x_pred(last, 0, 2)
             if t == 1:
                 prepare_d()
-            if first is not None:
-                for k in range(PACK if first == 0 else 2):
-                    first_matmul(first, k)
             if last is not None:
                 x_pred_scalar(last, 2)
             if second is not None:
@@ -372,7 +385,7 @@ def tile_originaltemporalsae_pa_t_kernel(tc, o, o_w, o_b, D, x, out_0, out_1):
                 regroup_r(cast)
                 r_quantised[cast] = quantise(r_grouped_of(cast))
             if first == 0:
-                bias_relu(first, 2, True)
-                bias_relu(first, 3, True)
+                for k in LATE:
+                    bias_relu(first, k, True)
             if new is not None:
                 o_quantised[new] = quantise(o_grouped_of(new))

@@ -212,6 +212,8 @@ def tile_originaltemporalsae_pa_t_kernel(tc, o, o_w, o_b, D, x, out_0, out_1):
         def second_matmul(u, tiles):
             codes, scales = r_quantised[u]
             out = bank()
+            if tiles[0] == 0:
+                nc.tensor.matmul(out[:], lhsT=zeros[:, 0:P], rhs=zeros[:], start=True, stop=True)
             for i, j in enumerate(tiles):
                 c = j * P
                 dz[u, j] = out[:, i * P : i * P + P]

@@ -207,7 +207,14 @@ def tile_originaltemporalsae_pa_t_kernel(tc, o, o_w, o_b, D, x, out_0, out_1):
                 nc.vector.tensor_copy(out=dst[:, 0:a, :], in_=src[:, 0:a, :])
                 nc.scalar.copy(out=dst[:, a:, :], in_=src[:, a:, :])
             else:
-                nc.gpsimd.tensor_scalar(out=dst, in0=src, scalar1=1.0, scalar2=0.0, op0=ALU.mult, op1=ALU.add)
+                nc.gpsimd.tensor_scalar(
+                    out=dst.rearrange("p (c i) t -> p c t i", i=4),
+                    in0=src.rearrange("p (c i) t -> p c t i", i=4),
+                    scalar1=1.0,
+                    scalar2=0.0,
+                    op0=ALU.mult,
+                    op1=ALU.add,
+                )
 
         def second_matmul(u, tiles):
             codes, scales = r_quantised[u]

@@ -238,7 +238,7 @@ def tile_originaltemporalsae_pa_t_kernel(tc, o, o_w, o_b, D, x, out_0, out_1):
         def square_sum(u, j):
             if u not in sum_sq:
                 sum_sq[u] = work.tile([P, UNIT], F32, tag="n2", name="n2")
-            squares = work.tile([P, P], F32, tag="junk_s", name="junk_s", bufs=2)
+            squares = work.tile([P, P], F32, tag="junk_s", name="junk_s", bufs=4)
             nc.scalar.activation(
                 out=squares[:], in_=dz[u, j], func=ACT.Square, accum_out=sum_sq[u][:, j : j + 1]
             )
@@ -254,7 +254,7 @@ def tile_originaltemporalsae_pa_t_kernel(tc, o, o_w, o_b, D, x, out_0, out_1):
         def dot_with_x(u, j):
             if u not in dot:
                 dot[u] = work.tile([P, UNIT], F32, tag="s", name="s")
-            products = work.tile([P, P], F32, tag="junk_v", name="junk_v", bufs=2)
+            products = work.tile([P, P], F32, tag="junk_v", name="junk_v", bufs=4)
             nc.vector.scalar_tensor_tensor(
                 out=products[:],
                 in0=dz[u, j],

@@ -60,7 +60,9 @@ def tile_originaltemporalsae_pa_t_kernel(tc, o, o_w, o_b, D, x, out_0, out_1):
             nc.tensor.matmul(bank()[:], lhsT=zeros[:, 0:P], rhs=zeros[:], start=True, stop=True)
 
         w_sb = const.tile([P, PACK, K], BF16, name="w_sb")
-        nc.sync.dma_start(out=w_sb[:], in_=o_w.rearrange("(a p) k -> p a k", p=P))
+        w_v = o_w.rearrange("(a p) k -> p a k", p=P)
+        for half in range(2):
+            nc.sync.dma_start(out=w_sb[:, 2 * half : 2 * half + 2, :], in_=w_v[:, 2 * half : 2 * half + 2, :])
         d_sb = const.tile([P, PACK, P], BF16, name="d_sb")
 
         o_tile = {}
@@ -366,7 +368,7 @@ def tile_originaltemporalsae_pa_t_kernel(tc, o, o_w, o_b, D, x, out_0, out_1):
                 for j in range(UNIT):
                     square_sum(second, j)
             if new is not None:
-                copy_o(new, 1, False)
+                copy_o(new, 1, new == 0)
             if last is not None:
                 x_pred(last, 0, 2)
             if t == 1:

from contextlib import ExitStack

import concourse.mybir as mybir
from concourse.masks import make_identity

F32 = mybir.dt.float32
BF16 = mybir.dt.bfloat16
U32 = mybir.dt.uint32
U8 = mybir.dt.uint8
FP8X4 = mybir.dt.float8_e4m3fn_x4
ACT = mybir.ActivationFunctionType
ALU = mybir.AluOpType

P = 128
K = 512
PACK = 4
TILES = 64
UNIT = 4
UNITS = TILES // UNIT
BANK = 512
EPS = 1e-6
TINY = 1e-30
FLOPS = 2 * 8192 * K * K + 2 * 8192 * K * P

O_LOADS = [2, 2, 4, 8, 8, 8, 8, 8, 8, 8]
WARM_UP = 4
VECTOR_ROWS = 352
X_LOAD = 16


def tile_originaltemporalsae_pa_t_kernel(tc, o, o_w, o_b, D, x, out_0, out_1):
    nc = tc.nc
    o_v = o.flatten_outer_dims().rearrange("(p i) k -> p i k", i=TILES)
    x_v = x.flatten_outer_dims().rearrange("(p i) k -> p i k", i=TILES)
    z_v = out_0.flatten_outer_dims().rearrange("(p i) f -> p i f", i=TILES)
    xp_v = out_1.flatten_outer_dims().rearrange("(p i) f -> p i f", i=TILES)

    with ExitStack() as ctx:
        const = ctx.enter_context(tc.tile_pool(name="const", bufs=1))
        work = ctx.enter_context(tc.tile_pool(name="work", bufs=3))
        psum = ctx.enter_context(tc.psum_pool(name="psum", bufs=8))
        ctx.enter_context(tc.manual_schedule())

        def bank():
            return psum.tile([P, BANK], F32, tag="bank", name="bank")

        zeros = const.tile([P, BANK], BF16, name="zeros")
        nc.vector.memset(zeros[:], 0.0)
        bias_rows = const.tile([P, P], BF16, name="bz")
        nc.vector.memset(bias_rows[:], 0.0)
        eps = const.tile([P, 1], F32, name="eps")
        nc.vector.memset(eps[:], EPS)
        tiny = const.tile([P, 1], F32, name="tiny")
        nc.vector.memset(tiny[:], TINY)
        warm = const.tile([P, 1], F32, name="warm")
        nc.scalar.activation(out=warm[:], in_=eps[:], func=ACT.Sqrt)
        ident = const.tile([P, P], F32, name="ident")
        make_identity(nc, ident[:])
        for i in range(WARM_UP):
            nc.tensor.matmul(bank()[:], lhsT=zeros[:, 0:P], rhs=zeros[:], start=True, stop=True)

        w_sb = const.tile([P, PACK, K], BF16, name="w_sb")
        w_v = o_w.rearrange("(a p) k -> p a k", p=P)
        for half in range(2):
            nc.sync.dma_start(out=w_sb[:, 2 * half : 2 * half + 2, :], in_=w_v[:, 2 * half : 2 * half + 2, :])
        d_sb = const.tile([P, PACK, P], BF16, name="d_sb")

        o_tile = {}
        x_tile = {}
        first = 0
        x_loads = 0
        for g, n in enumerate(O_LOADS):
            o_sb = const.tile([P, n, K], BF16, name="och%d" % g)
            nc.sync.dma_start(out=o_sb[:], in_=o_v[:, first : first + n, :])
            for l in range(n):
                o_tile[first + l] = o_sb[:, l, :]
            first += n
            if g == 1:
                nc.sync.dma_start(out=bias_rows[0:PACK, :], in_=o_b.rearrange("(t p) -> t p", p=P))
            if g == 2:
                nc.sync.dma_start(out=d_sb[:], in_=D.rearrange("(t p) j -> p t j", p=P))
            if g >= 2 and x_loads < TILES // X_LOAD:
                x_sb = const.tile([P, X_LOAD, P], BF16, name="xch%d" % x_loads)
                nc.sync.dma_start(out=x_sb[:], in_=x_v[:, X_LOAD * x_loads : X_LOAD * (x_loads + 1), :])
                for l in range(X_LOAD):
                    x_tile[X_LOAD * x_loads + l] = x_sb[:, l, :]
                x_loads += 1

        def transpose_words(rows0, rows1):
            words = bank()
            for j, rows in enumerate((rows0, rows1)):
                rows32 = rows.bitcast(F32)
                for u in range(2):
                    c = (2 * j + u) * P
                    nc.tensor.transpose(words[:, c : c + P], rows32[:, u * P : u * P + P], ident[:])
            return words

        def copy_words(grouped32, half, words, on_scalar):
            dst = grouped32[:, BANK * half : BANK * (half + 1)].rearrange("q (j r u) -> q j r u", j=2, u=2)
            src = words[:].rearrange("q (j u r) -> q j r u", j=2, u=2)
            if on_scalar:
                nc.scalar.copy(out=dst, in_=src)
            else:
                nc.vector.tensor_copy(out=dst, in_=src)

        bias_rows32 = const.tile([P, P], F32, name="bzf")
        bias = const.tile([P, PACK], F32, name="b_sb")
        d_grouped = const.tile([P, P, PACK], BF16, name="dg", align_bytes=64)
        d_codes = const.tile([P, P], U32, name="dc", align_bytes=64)
        d_scales = const.tile([P, P], U8, name="ds", align_bytes=64)

        def prepare_bias():
            bias_t = bank()
            nc.tensor.transpose(bias_t[:, 0:P], bias_rows32[:], ident[:])
            nc.vector.tensor_copy(out=bias[:], in_=bias_t[:, 0:PACK])

        def prepare_d():
            nc.vector.tensor_copy(out=d_grouped[:], in_=d_sb[:].rearrange("p t j -> p j t"))
            nc.vector.quantize_mx(
                out=d_codes[:].bitcast(FP8X4), scales=d_scales[:], in_=d_grouped[:].rearrange("p j t -> p (j t)")
            )

        w_grouped = const.tile([P, PACK * K], BF16, name="wg", align_bytes=64)
        for half in range(2):
            words = transpose_words(w_sb[:, 2 * half, :], w_sb[:, 2 * half + 1, :])
            copy_words(w_grouped[:].bitcast(F32), half, words, half == 1)
        nc.vector.tensor_copy(out=bias_rows32[:], in_=bias_rows[:])
        w_codes = const.tile([P, K], U32, name="wc", align_bytes=64)
        w_scales = const.tile([P, K], U8, name="ws", align_bytes=64)
        nc.vector.quantize_mx(out=w_codes[:].bitcast(FP8X4), scales=w_scales[:], in_=w_grouped[:])

        o_grouped = {}
        r_grouped = {}
        o_quantised = {}
        r_quantised = {}
        o_bank = {}
        d_bank = {}
        r_t = {}
        r_bank = {}
        dz = {}
        dz_bank = {}
        sum_sq = {}
        root = {}
        denom = {}
        inverse = {}
        dot = {}
        scale = {}
        z_sb = {}
        xp_sb = {}

        def o_grouped_of(u):
            if u not in o_grouped:
                o_grouped[u] = work.tile([P, PACK * K], BF16, tag="go", name="go", bufs=2, align_bytes=64)
            return o_grouped[u]

        def r_grouped_of(u):
            if u not in r_grouped:
                r_grouped[u] = work.tile([P, PACK * K], BF16, tag="gr", name="gr", bufs=1, align_bytes=64)
            return r_grouped[u]

        def transpose_o(u, half):
            row_tile = UNIT * u + 2 * half
            o_bank[u, half] = transpose_words(o_tile[row_tile], o_tile[row_tile + 1])

        def copy_o(u, half, on_scalar):
            copy_words(o_grouped_of(u)[:].bitcast(F32), half, o_bank[u, half], on_scalar)

        def quantise(grouped):
            codes = work.tile([P, K], U32, tag="cc", name="cc", bufs=5, align_bytes=64)
            scales = work.tile([P, K], U8, tag="sc", name="sc", bufs=5, align_bytes=64)
            nc.vector.quantize_mx(out=codes[:].bitcast(FP8X4), scales=scales[:], in_=grouped[:])
            return codes, scales

        def first_matmul(u, t):
            codes, scales = o_quantised[u]
            d_bank[u, t] = bank()
            nc.tensor.matmul_mx(
                out=d_bank[u, t][:],
                lhsT=w_codes[:, t * P : t * P + P].bitcast(FP8X4),
                lhsT_scale=w_scales[:, t * P : t * P + P],
                rhs=codes[:].bitcast(FP8X4),
                rhs_scale=scales[:],
                start=True,
                stop=True,
            )

        def bias_relu(u, t, on_scalar):
            if u not in r_t:
                r_t[u] = work.tile([P, PACK, K], F32, tag="rt", name="rt", bufs=4)
            if not on_scalar:
                nc.vector.tensor_scalar(
                    out=r_t[u][:, t, :],
                    in0=d_bank[u, t][:],
                    scalar1=bias[:, t : t + 1],
                    scalar2=0.0,
                    op0=ALU.add,
                    op1=ALU.max,
                )
            else:
                nc.scalar.activation(
                    out=r_t[u][:, t, :], in_=d_bank[u, t][:], func=ACT.Relu, bias=bias[:, t : t + 1], scale=1.0
                )

        def regroup_r(u):
            dst = r_grouped_of(u)[:].rearrange("p (c t) -> p c t", t=PACK)
            src = r_t[u][:].rearrange("p t c -> p c t")
            if u == 0:
                a = VECTOR_ROWS
                nc.vector.tensor_copy(out=dst[:, 0:a, :], in_=src[:, 0:a, :])
                nc.scalar.copy(out=dst[:, a:, :], in_=src[:, a:, :])
            else:
                nc.gpsimd.tensor_scalar(
                    out=dst.rearrange("p (c i) t -> p c t i", i=4),
                    in0=src.rearrange("p (c i) t -> p c t i", i=4),
                    scalar1=1.0,
                    scalar2=0.0,
                    op0=ALU.mult,
                    op1=ALU.add,
                )

        def second_matmul(u, tiles):
            codes, scales = r_quantised[u]
            out = bank()
            if tiles[0] == 0:
                nc.tensor.matmul(out[:], lhsT=zeros[:, 0:P], rhs=zeros[:], start=True, stop=True)
            for i, j in enumerate(tiles):
                c = j * P
                dz[u, j] = out[:, i * P : i * P + P]
                nc.tensor.matmul_mx(
                    out=dz[u, j],
                    lhsT=codes[:, c : c + P].bitcast(FP8X4),
                    lhsT_scale=scales[:, c : c + P],
                    rhs=d_codes[:].bitcast(FP8X4),
                    rhs_scale=d_scales[:],
                    start=True,
                    stop=True,
                )
            dz_bank[u, tiles[0]] = out

        def square_sum(u, j):
            if u not in sum_sq:
                sum_sq[u] = work.tile([P, UNIT], F32, tag="n2", name="n2")
            squares = work.tile([P, P], F32, tag="junk_s", name="junk_s", bufs=4)
            nc.scalar.activation(
                out=squares[:], in_=dz[u, j], func=ACT.Square, accum_out=sum_sq[u][:, j : j + 1]
            )

        def take_root(u):
            root[u] = work.tile([P, UNIT], F32, tag="nr", name="nr")
            nc.scalar.activation(out=root[u][:], in_=sum_sq[u][:], func=ACT.Sqrt, bias=tiny[:, 0:1], scale=1.0)

        def denominator(u):
            denom[u] = work.tile([P, UNIT], F32, tag="den", name="den")
            nc.scalar.activation(out=denom[u][:], in_=root[u][:], func=ACT.Square, bias=eps[:, 0:1], scale=1.0)

        def dot_with_x(u, j):
            if u not in dot:
                dot[u] = work.tile([P, UNIT], F32, tag="s", name="s")
            products = work.tile([P, P], F32, tag="junk_v", name="junk_v", bufs=4)
            nc.vector.scalar_tensor_tensor(
                out=products[:],
                in0=dz[u, j],
                scalar=1.0,
                in1=x_tile[UNIT * u + j],
                op0=ALU.mult,
                op1=ALU.mult,
                accum_out=dot[u][:, j : j + 1],
            )

        def invert(u):
            inverse[u] = work.tile([P, UNIT], F32, tag="rec", name="rec")
            nc.vector.reciprocal(out=inverse[u][:], in_=denom[u][:])

        def projection_scale(u):
            scale[u] = work.tile([P, UNIT], F32, tag="pp", name="pp")
            nc.vector.tensor_tensor(out=scale[u][:], in0=dot[u][:], in1=inverse[u][:], op=ALU.mult)

        def x_pred(u, j, n):
            if u not in xp_sb:
                xp_sb[u] = work.tile([P, UNIT, P], F32, tag="xp", name="xp", bufs=4)
            nc.vector.tensor_tensor(
                out=xp_sb[u][:, j : j + n, :],
                in0=dz_bank[u, j][:, 0 : n * P].rearrange("p (j c) -> p j c", j=n),
                in1=scale[u][:, j : j + n].unsqueeze(2).to_broadcast([P, n, P]),
                op=ALU.mult,
            )
            if u >= UNITS - 2:
                nc.sync.dma_start(out=xp_v[:, UNIT * u + j : UNIT * u + j + n, :], in_=xp_sb[u][:, j : j + n, :])

        def x_pred_scalar(u, j):
            if u not in xp_sb:
                xp_sb[u] = work.tile([P, UNIT, P], F32, tag="xp", name="xp", bufs=4)
            nc.scalar.activation(out=xp_sb[u][:, j, :], in_=dz[u, j], func=ACT.Copy, scale=scale[u][:, j : j + 1])
            if u >= UNITS - 2:
                nc.sync.dma_start(out=xp_v[:, UNIT * u + j, :], in_=xp_sb[u][:, j, :])

        def transpose_r(u, j):
            r_bank[u, j] = bank()
            for t in range(PACK):
                nc.tensor.transpose(
                    r_bank[u, j][:, t * P : t * P + P], r_t[u][:, t, j * P : j * P + P], ident[:]
                )

        def z_pred(u, j, on_scalar):
            if u not in z_sb:
                z_sb[u] = work.tile([P, UNIT, K], F32, tag="zs", name="zs", bufs=4)
            p = scale[u][:, j : j + 1]
            if on_scalar:
                nc.scalar.activation(out=z_sb[u][:, j, :], in_=r_bank[u, j][:], func=ACT.Copy, scale=p)
            else:
                nc.vector.tensor_scalar(
                    out=z_sb[u][:, j, :], in0=r_bank[u, j][:], scalar1=p, scalar2=None, op0=ALU.mult
                )
            if u >= UNITS - 2:
                nc.sync.dma_start(out=z_v[:, UNIT * u + j, :], in_=z_sb[u][:, j, :])

        def store(u):
            if u < UNITS - 2:
                nc.sync.dma_start(out=z_v[:, UNIT * u : UNIT * u + UNIT, :], in_=z_sb[u][:])
                nc.sync.dma_start(out=xp_v[:, UNIT * u : UNIT * u + UNIT, :], in_=xp_sb[u][:])

        def live(u):
            return 0 <= u < UNITS

        for t in range(UNITS + 4):
            LATE = (2, 3)
            new, first, cast, second, last = (t - i if live(t - i) else None for i in range(5))
            if cast == 0:
                regroup_r(cast)
                r_quantised[cast] = quantise(r_grouped_of(cast))
            if new is not None:
                transpose_o(new, 0)
            if cast is not None and cast > 0:
                for k in LATE:
                    first_matmul(cast, k)
            if last is not None:
                transpose_r(last, 0)
            if last is not None:
                transpose_r(last, 1)
            if last is not None:
                transpose_r(last, 2)
            if last is not None:
                transpose_r(last, 3)
            if new is not None:
                transpose_o(new, 1)
            if second is not None:
                second_matmul(second, (0, 1))
            if second is not None:
                second_matmul(second, (2, 3))
            if first is not None:
                for k in (1, 0, 2, 3):
                    if first == 0 or k not in LATE:
                        first_matmul(first, k)
            if t == 0:
                prepare_bias()
            if cast is not None and cast > 0:
                for k in LATE:
                    bias_relu(cast, k, True)
            if last is not None:
                z_pred(last, 1, True)
            if new is not None:
                copy_o(new, 0, True)
            if last is not None:
                z_pred(last, 0, False)
                z_pred(last, 2, False)
                z_pred(last, 3, True)
            if second is not None:
                for j in range(UNIT):
                    square_sum(second, j)
            if new is not None:
                copy_o(new, 1, new == 0)
            if last is not None:
                x_pred(last, 0, 2)
            if t == 1:
                prepare_d()
            if last is not None:
                x_pred_scalar(last, 2)
            if second is not None:
                take_root(second)
            if last is not None:
                x_pred_scalar(last, 3)
                store(last)
            if second is not None:
                denominator(second)
            if first is not None:
                bias_relu(first, 1, True)
            if second is not None:
                for j in range(UNIT):
                    dot_with_x(second, j)
                invert(second)
            if first is not None:
                bias_relu(first, 0, False)
            if second is not None:
                projection_scale(second)
            if cast is not None and cast > 0:
                regroup_r(cast)
                r_quantised[cast] = quantise(r_grouped_of(cast))
            if first == 0:
                for k in LATE:
                    bias_relu(first, k, True)
            if new is not None:
                o_quantised[new] = quantise(o_grouped_of(new))
